import numpy as np
import ml_dtypes


def mxq(x, axis, fmt="e4m3"):
    dtype, down = {"e4m3": (ml_dtypes.float8_e4m3fn, 7), "e5m2": (ml_dtypes.float8_e5m2, 14)}[fmt]
    v = np.moveaxis(np.asarray(x, np.float32).astype(ml_dtypes.bfloat16).astype(np.float64), axis, -1)
    blocks = v.reshape(v.shape[:-1] + (-1, 32))
    amax = np.abs(blocks).max(-1, keepdims=True)
    byte = np.maximum(np.where(amax > 0, np.frexp(amax)[1] - 1 + 127, 0) - down, 1)
    scale = np.exp2(byte - 127.0)
    codes = (blocks / scale).astype(np.float32).astype(dtype).astype(np.float64)
    return np.moveaxis((codes * scale).reshape(v.shape), -1, axis)


WIDE = False


def mx_kscale(k):
    if not WIDE:
        return np.ones(k)
    levels = np.array([10, -10, 5, -5, 0])
    a = np.random.permutation(np.resize(levels, k // 512 * 4)).reshape(k // 512, 4)
    idx = np.arange(k)
    return np.exp2(a[idx // 512, idx % 128 // 32])


BF16 = ml_dtypes.bfloat16


def bf(x):
    return np.asarray(x, np.float32).astype(BF16)


def f64(x):
    return np.asarray(x).astype(np.float64)


B, T, N, D, KD, VD = 2, 1024, 1024, 512, 512, 512
ITERS = 5
REG = 1.0
SIG = 3.5


def lse(x, axis):
    m = x.max(axis=axis, keepdims=True)
    return m + np.log(np.exp(x - m).sum(axis=axis, keepdims=True))


def setup_inputs():
    s = mx_kscale(VD)
    return {"q_proj": bf(np.random.standard_normal((T, D)) * SIG),
            "k_proj": bf(np.random.standard_normal((B, N, D)) * SIG),
            "v": bf(np.random.standard_normal((B, N, VD)) * s),
            "w_v": bf(np.random.standard_normal((VD, D)) * 1.5 / np.sqrt(VD) / s[:, None])}


def reference(q_proj, k_proj, v, w_v):
    q2 = (f64(q_proj) * f64(q_proj)).sum(-1)
    k2 = (f64(k_proj) * f64(k_proj)).sum(-1)
    qk = f64(q_proj) @ f64(k_proj).transpose(0, 2, 1)
    sq = q2[None, :, None] + k2[:, None, :] - 2.0 * qk
    logk = -np.sqrt(np.maximum(sq, 0.0)) / REG
    log_a = -np.log(N)
    log_b = 0.0
    g = np.zeros((B, T, 1))
    for _ in range(ITERS):
        f = log_a - lse(logk + g, 1)
        g = log_b - lse(logk + f, 2)
    pi = np.exp(logk + f + g)
    vp = mxq(f64(v), 2, "e4m3") @ mxq(f64(w_v), 0, "e4m3")
    return mxq(pi, 2, "e4m3") @ mxq(vp, 1, "e4m3")

@@ -1,0 +1,273 @@
+from contextlib import ExitStack
+
+import concourse.mybir as mybir
+from concourse.masks import make_identity
+
+F32 = mybir.dt.float32
+BF16 = mybir.dt.bfloat16
+U32 = mybir.dt.uint32
+U8 = mybir.dt.uint8
+FP8X4 = mybir.dt.float8_e4m3fn_x4
+ALU = mybir.AluOpType
+ACT = mybir.ActivationFunctionType
+AX = mybir.AxisListType
+
+P = 128
+B = 2
+T = 1024
+N = 1024
+D = 512
+ITERS = 5
+TINY = 2.0 ** -100
+FLOPS = 2 * B * T * N * D + 2 * B * N * D * D + 2 * B * T * N * D
+
+
+def tile_sinkhornattention_pa_kernel(tc, q_proj, k_proj, v, w_v, out):
+    nc = tc.nc
+    with ExitStack() as ctx:
+        const = ctx.enter_context(tc.tile_pool(name="const", bufs=1))
+        big = ctx.enter_context(tc.tile_pool(name="big", bufs=1))
+        scr = ctx.enter_context(tc.tile_pool(name="scr", bufs=2))
+        small = ctx.enter_context(tc.tile_pool(name="small", bufs=2))
+        psum = ctx.enter_context(tc.psum_pool(name="psum", bufs=1))
+
+        ident_bf = const.tile([P, P], BF16, name="ident_bf")
+        make_identity(nc, ident_bf[:])
+        ident_f = const.tile([P, P], F32, name="ident_f")
+        make_identity(nc, ident_f[:])
+
+        q_raw = big.tile([P, 8, D], BF16, name="q_raw", tag="sA", align_bytes=64)
+        k_raw = [
+            big.tile([P, 8, D], BF16, name="k_raw0", tag="sB", align_bytes=64),
+            big.tile([P, 8, D], BF16, name="k_raw1", tag="sC", align_bytes=64),
+        ]
+        qv = q_proj.rearrange("(p i) d -> p i d", i=8)
+        kv = [k_proj[b].rearrange("(c p j) d -> p c j d", c=2, j=4) for b in range(B)]
+        nc.sync.dma_start(out=q_raw[:, 0:4, :], in_=qv[:, 0:4, :])
+        nc.sync.dma_start(out=k_raw[0][:, 0:4, :], in_=kv[0][:, 0, :, :])
+        nc.sync.dma_start(out=q_raw[:, 4:8, :], in_=qv[:, 4:8, :])
+        nc.sync.dma_start(out=k_raw[0][:, 4:8, :], in_=kv[0][:, 1, :, :])
+        nc.sync.dma_start(out=k_raw[1][:, 0:4, :], in_=kv[1][:, 0, :, :])
+        nc.sync.dma_start(out=k_raw[1][:, 4:8, :], in_=kv[1][:, 1, :, :])
+
+        qT = big.tile([P, 4, T], BF16, name="qT", tag="sD", align_bytes=64)
+        kT = [
+            big.tile([P, 4, N], BF16, name="kT0", tag="sE", align_bytes=64),
+            big.tile([P, 4, N], BF16, name="kT1", tag="sF", align_bytes=64),
+        ]
+        q2 = const.tile([P, 8], F32, name="q2")
+        k2 = [const.tile([P, 8], F32, name="k2_%d" % b) for b in range(B)]
+        q2b = big.tile([P, T], F32, name="q2b", tag="sG", align_bytes=64)
+
+        for i in range(8):
+            jq = scr.tile([P, D], F32, name="jq", tag="jq")
+            nc.vector.scalar_tensor_tensor(
+                out=jq[:], in0=q_raw[:, i, :], scalar=1.0, in1=q_raw[:, i, :],
+                op0=ALU.mult, op1=ALU.mult, accum_out=q2[:, i:i + 1])
+
+        def k_norms(b):
+            for cj in range(8):
+                jk = scr.tile([P, D], F32, name="jk", tag="jk")
+                nc.scalar.activation(out=jk[:], in_=k_raw[b][:, cj, :], func=ACT.Square,
+                                     accum_out=k2[b][:, cj:cj + 1])
+
+        k_norms(0)
+
+        for i in range(8):
+            pt = psum.tile([P, 4, P], BF16, name="pt", tag="tr", bufs=2)
+            for dk in range(4):
+                nc.tensor.transpose(out=pt[:, dk, :], in_=q_raw[:, i, P * dk:P * dk + P],
+                                    identity=ident_bf[:])
+            nc.vector.tensor_scalar(out=qT[:, :, P * i:P * i + P], in0=pt[:], scalar1=-2.0,
+                                    scalar2=None, op0=ALU.mult)
+
+        def k_transposes(b):
+            for cj in range(8):
+                pt = psum.tile([P, 4, P], BF16, name="pt", tag="tr", bufs=2)
+                for dk in range(4):
+                    nc.tensor.transpose(out=pt[:, dk, :], in_=k_raw[b][:, cj, P * dk:P * dk + P],
+                                        identity=ident_bf[:])
+                if cj % 2 == 0:
+                    nc.scalar.copy(out=kT[b][:, :, P * cj:P * cj + P], in_=pt[:])
+                else:
+                    nc.vector.tensor_copy(out=kT[b][:, :, P * cj:P * cj + P], in_=pt[:])
+
+        k_transposes(0)
+
+        def spread(vec, dst):
+            for hh in range(2):
+                pb = psum.tile([P, 512], F32, name="pb", tag="tr", bufs=2)
+                for a in range(4):
+                    i = 4 * hh + a
+                    nc.tensor.transpose(out=pb[:, P * a:P * a + P],
+                                        in_=vec[:, i:i + 1].to_broadcast([P, P]),
+                                        identity=ident_f[:])
+                nc.scalar.copy(out=dst[:, 512 * hh:512 * hh + 512], in_=pb[:])
+
+        spread(q2, q2b)
+
+        F = [big.tile([P, 8, T], F32, name="F%d" % b, tag="F%d" % b) for b in range(B)]
+        TH = [big.tile([P, 8, T], BF16, name="TH%d" % b, tag="th%d" % b, align_bytes=64) for b in range(B)]
+        TL = [big.tile([P, 8, T], BF16, name="TL%d" % b, tag="tl%d" % b, align_bytes=64) for b in range(B)]
+        minsq = [const.tile([P, 8], F32, name="minsq%d" % b) for b in range(B)]
+        mn = [const.tile([P, 8], F32, name="mn%d" % b) for b in range(B)]
+        S = [None, None]
+
+        def phase1(b):
+            for cj in range(8):
+                for h in range(2):
+                    pq = psum.tile([P, 512], F32, name="pq", tag="mm", bufs=4)
+                    for dk in range(4):
+                        nc.tensor.matmul(out=pq[:], lhsT=kT[b][:, dk, P * cj:P * cj + P],
+                                         rhs=qT[:, dk, 512 * h:512 * h + 512],
+                                         start=(dk == 0), stop=(dk == 3))
+                    nc.vector.scalar_tensor_tensor(
+                        out=F[b][:, cj, 512 * h:512 * h + 512], in0=pq[:],
+                        scalar=k2[b][:, cj:cj + 1], in1=q2b[:, 512 * h:512 * h + 512],
+                        op0=ALU.add, op1=ALU.add)
+                nc.vector.tensor_scalar(out=F[b][:, cj, :], in0=F[b][:, cj, :], scalar1=TINY,
+                                        scalar2=None, op0=ALU.max, op1=ALU.min,
+                                        accum_out=minsq[b][:, cj:cj + 1])
+                nc.scalar.activation(out=F[b][:, cj, :], in_=F[b][:, cj, :], func=ACT.Sqrt)
+            nc.scalar.activation(out=mn[b][:], in_=minsq[b][:], func=ACT.Sqrt)
+            S[b] = small.tile([P, 8], F32, name="S%d" % b, tag="S%d" % b)
+            for cj in range(8):
+                nc.scalar.activation(out=F[b][:, cj, :], in_=F[b][:, cj, :], func=ACT.Exp,
+                                     bias=mn[b][:, cj:cj + 1], scale=-1.0,
+                                     accum_out=S[b][:, cj:cj + 1])
+                nc.gpsimd.tensor_scalar(out=TH[b][:, cj, :], in0=F[b][:, cj, :], scalar1=1.0,
+                                        scalar2=0.0, op0=ALU.mult, op1=ALU.add)
+                lo_eng = nc.vector if cj % 2 == 0 else nc.gpsimd
+                lo_eng.tensor_tensor(out=TL[b][:, cj, :], in0=F[b][:, cj, :],
+                                     in1=TH[b][:, cj, :], op=ALU.subtract)
+
+        phase1(0)
+        k_norms(1)
+        k_transposes(1)
+        phase1(1)
+
+        w_raw = big.tile([P, 4, D], BF16, name="w_raw", tag="sE", align_bytes=64)
+        nc.sync.dma_start(out=w_raw[:].rearrange("p (u e) c -> p u e c", u=2),
+                          in_=w_v.rearrange("(u q e) c -> q u e c", u=2, e=2))
+        wg = big.tile([P, D, 4], BF16, name="wg", tag="sF", align_bytes=64)
+        nc.vector.tensor_copy(out=wg[:], in_=w_raw[:].rearrange("p t c -> p c t"))
+        wc = const.tile([P, D], U32, name="wc", align_bytes=64)
+        ws = const.tile([P, D], U8, name="ws", align_bytes=64)
+        nc.vector.quantize_mx(out=wc[:].bitcast(FP8X4), scales=ws[:],
+                              in_=wg[:].rearrange("p c t -> p (c t)"))
+        vpc = [const.tile([P, 2, D], U32, name="vpc%d" % b, align_bytes=64) for b in range(B)]
+        vps = [const.tile([P, 2, D], U8, name="vps%d" % b, align_bytes=64) for b in range(B)]
+
+        def value_path(b):
+            v_raw = big.tile([P, 8, D], BF16, name="v_raw", tag=("sA", "sB")[b], align_bytes=64)
+            nc.sync.dma_start(out=v_raw[:].rearrange("p (c j) d -> p c j d", c=2),
+                              in_=v[b].rearrange("(c p j) d -> p c j d", c=2, j=4))
+            vw = v_raw[:].bitcast(F32)
+            vg = big.tile([P, N, 4], BF16, name="vg", tag="sC", align_bytes=64)
+            vgw = vg[:].bitcast(F32)
+            for g in range(4):
+                pv = psum.tile([P, 2, 2, P], F32, name="pv", tag="tr", bufs=2)
+                for a in range(2):
+                    for u in range(2):
+                        nc.tensor.transpose(out=pv[:, a, u, :],
+                                            in_=vw[:, 2 * g + a, P * u:P * u + P],
+                                            identity=ident_f[:])
+                nc.scalar.copy(
+                    out=vgw[:, 256 * g:256 * g + 256, :].rearrange("p (a n) u -> p a n u", a=2),
+                    in_=pv[:].rearrange("p a u n -> p a n u"))
+            vc = big.tile([P, N], U32, name="vc", tag="vc", align_bytes=64)
+            vs_ = big.tile([P, N], U8, name="vs_", tag="vs_", align_bytes=64)
+            nc.vector.quantize_mx(out=vc[:].bitcast(FP8X4), scales=vs_[:],
+                                  in_=vg[:].rearrange("p n t -> p (n t)"))
+            vpg = big.tile([P, 2, D, 4], BF16, name="vpg", tag="sD", align_bytes=64)
+            for c in range(2):
+                for eq in range(4):
+                    pvp = psum.tile([P, 4, P], F32, name="pvp", tag="mm", bufs=4)
+                    for j in range(4):
+                        cj = 4 * c + j
+                        nc.tensor.matmul_mx(
+                            out=pvp[:, j, :],
+                            lhsT=vc[:, P * cj:P * cj + P].bitcast(FP8X4),
+                            lhsT_scale=vs_[:, P * cj:P * cj + P],
+                            rhs=wc[:, P * eq:P * eq + P].bitcast(FP8X4),
+                            rhs_scale=ws[:, P * eq:P * eq + P],
+                            start=True, stop=True)
+                    nc.scalar.copy(out=vpg[:, c, P * eq:P * eq + P, :],
+                                   in_=pvp[:].rearrange("p j e -> p e j"))
+            nc.vector.quantize_mx(out=vpc[b][:].rearrange("p c e -> p (c e)").bitcast(FP8X4),
+                                  scales=vps[b][:].rearrange("p c e -> p (c e)"),
+                                  in_=vpg[:].rearrange("p c e j -> p (c e j)"))
+
+        junk = big.tile([P, T], F32, name="junk", tag="sG", align_bytes=64)
+        ub = [big.tile([P, T], F32, name="ub%d" % b, tag="ub%d" % b) for b in range(B)]
+        vcur = [None, None]
+        for it in range(ITERS):
+            vsp = [None, None]
+            for b in range(B):
+                with tc.high_priority():
+                    vcur[b] = small.tile([P, 8], F32, name="v%d" % b, tag="v%d" % b)
+                    nc.vector.reciprocal(out=vcur[b][:], in_=S[b][:])
+                    vsp[b] = small.tile([P, 8, 2], BF16, name="vsp%d" % b, tag="vsp%d" % b)
+                    nc.vector.tensor_copy(out=vsp[b][:, :, 0], in_=vcur[b][:])
+                    nc.vector.tensor_tensor(out=vsp[b][:, :, 1], in0=vcur[b][:],
+                                            in1=vsp[b][:, :, 0], op=ALU.subtract)
+                    R = psum.tile([P, 8, 2], F32, name="R", tag="mv", bufs=2)
+                    for i in range(8):
+                        idx = 0
+                        for cj in range(8):
+                            for piece in (TH[b], TL[b]):
+                                nc.tensor.matmul(out=R[:, i, :],
+                                                 lhsT=piece[:, cj, P * i:P * i + P],
+                                                 rhs=vsp[b][:, cj, :],
+                                                 start=(idx == 0), stop=(idx == 15))
+                                idx += 1
+                    r = small.tile([P, 8], F32, name="r%d" % b, tag="r%d" % b)
+                    nc.vector.tensor_reduce(out=r[:], in_=R[:], axis=AX.X, op=ALU.add)
+                    u = small.tile([P, 8], F32, name="u%d" % b, tag="u%d" % b)
+                    nc.vector.reciprocal(out=u[:], in_=r[:])
+                    spread(u, ub[b])
+                if it == ITERS - 1:
+                    for cj in range(8):
+                        nc.scalar.activation(out=F[b][:, cj, :], in_=F[b][:, cj, :], func=ACT.Copy,
+                                             scale=vcur[b][:, cj:cj + 1])
+            if it < ITERS - 1:
+                for b in range(B):
+                    S[b] = small.tile([P, 8], F32, name="S%d" % b, tag="S%d" % b)
+                    for cj in range(8):
+                        nc.vector.scalar_tensor_tensor(
+                            out=junk[:], in0=F[b][:, cj, :], scalar=1.0, in1=ub[b][:],
+                            op0=ALU.mult, op1=ALU.mult, accum_out=S[b][:, cj:cj + 1])
+
+        value_path(0)
+        value_path(1)
+
+        for b in range(B):
+            pig = big.tile([P, 2, T, 4], BF16, name="pig%d" % b, tag="th%d" % b, align_bytes=64)
+            pic = big.tile([P, 2, T], U32, name="pic%d" % b, tag="tl%d" % b, align_bytes=64)
+            pis = const.tile([P, 2, T], U8, name="pis%d" % b, align_bytes=64)
+            ov = out[b].rearrange("(p i) d -> p i d", i=8)
+            for h in range(2):
+                sl = slice(512 * h, 512 * h + 512)
+                for c in range(2):
+                    nc.vector.tensor_tensor(
+                        out=pig[:, c, sl, :],
+                        in0=F[b][:, 4 * c:4 * c + 4, sl].rearrange("p j t -> p t j"),
+                        in1=ub[b][:, sl].unsqueeze(2).to_broadcast([P, 512, 4]),
+                        op=ALU.mult)
+                for c in range(2):
+                    nc.vector.quantize_mx(out=pic[:, c, sl].bitcast(FP8X4), scales=pis[:, c, sl],
+                                          in_=pig[:, c, sl, :].rearrange("p t j -> p (t j)"))
+                ost = big.tile([P, 4, D], F32, name="ost", tag=("sA", "sB")[h], align_bytes=64)
+                for a in range(4):
+                    i = 4 * h + a
+                    po = psum.tile([P, D], F32, name="po", tag="mm", bufs=4)
+                    for c in range(2):
+                        nc.tensor.matmul_mx(
+                            out=po[:],
+                            lhsT=pic[:, c, P * i:P * i + P].bitcast(FP8X4),
+                            lhsT_scale=pis[:, c, P * i:P * i + P],
+                            rhs=vpc[b][:, c, :].bitcast(FP8X4),
+                            rhs_scale=vps[b][:, c, :],
+                            start=(c == 0), stop=(c == 1))
+                    nc.scalar.copy(out=ost[:, a, :], in_=po[:])
+                nc.sync.dma_start(out=ov[:, 4 * h:4 * h + 4, :], in_=ost[:])

@@ -21,10 +21,13 @@ ITERS = 5
 TINY = 2.0 ** -100
 FLOPS = 2 * B * T * N * D + 2 * B * N * D * D + 2 * B * T * N * D
 
+XPE = 3
+
 
 def tile_sinkhornattention_pa_kernel(tc, q_proj, k_proj, v, w_v, out):
     nc = tc.nc
     with ExitStack() as ctx:
+        ctx.enter_context(tc.manual_schedule())
         const = ctx.enter_context(tc.tile_pool(name="const", bufs=1))
         big = ctx.enter_context(tc.tile_pool(name="big", bufs=1))
         scr = ctx.enter_context(tc.tile_pool(name="scr", bufs=2))
@@ -38,135 +41,262 @@ def tile_sinkhornattention_pa_kernel(tc, q_proj, k_proj, v, w_v, out):
 
         q_raw = big.tile([P, 8, D], BF16, name="q_raw", tag="sA", align_bytes=64)
         k_raw = [
-            big.tile([P, 8, D], BF16, name="k_raw0", tag="sB", align_bytes=64),
-            big.tile([P, 8, D], BF16, name="k_raw1", tag="sC", align_bytes=64),
+            [big.tile([P, 4, D], BF16, name="k_raw0%d" % c, tag="b%d" % c, align_bytes=64) for c in range(2)],
         ]
-        qv = q_proj.rearrange("(p i) d -> p i d", i=8)
-        kv = [k_proj[b].rearrange("(c p j) d -> p c j d", c=2, j=4) for b in range(B)]
-        nc.sync.dma_start(out=q_raw[:, 0:4, :], in_=qv[:, 0:4, :])
-        nc.sync.dma_start(out=k_raw[0][:, 0:4, :], in_=kv[0][:, 0, :, :])
-        nc.sync.dma_start(out=q_raw[:, 4:8, :], in_=qv[:, 4:8, :])
-        nc.sync.dma_start(out=k_raw[0][:, 4:8, :], in_=kv[0][:, 1, :, :])
-        nc.sync.dma_start(out=k_raw[1][:, 0:4, :], in_=kv[1][:, 0, :, :])
-        nc.sync.dma_start(out=k_raw[1][:, 4:8, :], in_=kv[1][:, 1, :, :])
-
-        qT = big.tile([P, 4, T], BF16, name="qT", tag="sD", align_bytes=64)
+        k_raw1 = big.tile([P, 8, D], BF16, name="k_raw1", tag="sC", align_bytes=64)
+        k_raw.append([k_raw1[:, 0:4, :], k_raw1[:, 4:8, :]])
+        qT = [big.tile([P, 2, T], BF16, name="qT%d" % s, tag="d%d" % s, align_bytes=64) for s in range(2)]
         kT = [
-            big.tile([P, 4, N], BF16, name="kT0", tag="sE", align_bytes=64),
-            big.tile([P, 4, N], BF16, name="kT1", tag="sF", align_bytes=64),
+            [big.tile([P, 2, N], BF16, name="kT0%d" % s, tag="e%d" % s, align_bytes=64) for s in range(2)],
+            [big.tile([P, 2, N], BF16, name="kT1%d" % s, tag="f%d" % s, align_bytes=64) for s in range(2)],
         ]
         q2 = const.tile([P, 8], F32, name="q2")
         k2 = [const.tile([P, 8], F32, name="k2_%d" % b) for b in range(B)]
         q2b = big.tile([P, T], F32, name="q2b", tag="sG", align_bytes=64)
-
-        for i in range(8):
-            jq = scr.tile([P, D], F32, name="jq", tag="jq")
-            nc.vector.scalar_tensor_tensor(
-                out=jq[:], in0=q_raw[:, i, :], scalar=1.0, in1=q_raw[:, i, :],
-                op0=ALU.mult, op1=ALU.mult, accum_out=q2[:, i:i + 1])
-
-        def k_norms(b):
-            for cj in range(8):
-                jk = scr.tile([P, D], F32, name="jk", tag="jk")
-                nc.scalar.activation(out=jk[:], in_=k_raw[b][:, cj, :], func=ACT.Square,
-                                     accum_out=k2[b][:, cj:cj + 1])
-
-        k_norms(0)
-
-        for i in range(8):
-            pt = psum.tile([P, 4, P], BF16, name="pt", tag="tr", bufs=2)
-            for dk in range(4):
-                nc.tensor.transpose(out=pt[:, dk, :], in_=q_raw[:, i, P * dk:P * dk + P],
-                                    identity=ident_bf[:])
-            nc.vector.tensor_scalar(out=qT[:, :, P * i:P * i + P], in0=pt[:], scalar1=-2.0,
-                                    scalar2=None, op0=ALU.mult)
-
-        def k_transposes(b):
-            for cj in range(8):
-                pt = psum.tile([P, 4, P], BF16, name="pt", tag="tr", bufs=2)
-                for dk in range(4):
-                    nc.tensor.transpose(out=pt[:, dk, :], in_=k_raw[b][:, cj, P * dk:P * dk + P],
-                                        identity=ident_bf[:])
-                if cj % 2 == 0:
-                    nc.scalar.copy(out=kT[b][:, :, P * cj:P * cj + P], in_=pt[:])
-                else:
-                    nc.vector.tensor_copy(out=kT[b][:, :, P * cj:P * cj + P], in_=pt[:])
-
-        k_transposes(0)
-
-        def spread(vec, dst):
-            for hh in range(2):
-                pb = psum.tile([P, 512], F32, name="pb", tag="tr", bufs=2)
-                for a in range(4):
-                    i = 4 * hh + a
-                    nc.tensor.transpose(out=pb[:, P * a:P * a + P],
-                                        in_=vec[:, i:i + 1].to_broadcast([P, P]),
-                                        identity=ident_f[:])
-                nc.scalar.copy(out=dst[:, 512 * hh:512 * hh + 512], in_=pb[:])
-
-        spread(q2, q2b)
-
         F = [big.tile([P, 8, T], F32, name="F%d" % b, tag="F%d" % b) for b in range(B)]
         TH = [big.tile([P, 8, T], BF16, name="TH%d" % b, tag="th%d" % b, align_bytes=64) for b in range(B)]
         TL = [big.tile([P, 8, T], BF16, name="TL%d" % b, tag="tl%d" % b, align_bytes=64) for b in range(B)]
         minsq = [const.tile([P, 8], F32, name="minsq%d" % b) for b in range(B)]
         mn = [const.tile([P, 8], F32, name="mn%d" % b) for b in range(B)]
+        ub = [big.tile([P, T], F32, name="ub%d" % b, tag="ub%d" % b) for b in range(B)]
+        NHL = [[None] * XPE, [None] * XPE]
+        NHL_TAGS = (("e0", "e1", "d0"), ("d1", "f0", "f1"))
         S = [None, None]
+        vcur = [None, None]
+        vsp = [None, None]
+        usp = [None, None]
+        Rt = [None, None]
+        Sp = [None, None]
+        ucur = [None, None]
 
-        def phase1(b):
-            for cj in range(8):
-                for h in range(2):
-                    pq = psum.tile([P, 512], F32, name="pq", tag="mm", bufs=4)
-                    for dk in range(4):
-                        nc.tensor.matmul(out=pq[:], lhsT=kT[b][:, dk, P * cj:P * cj + P],
-                                         rhs=qT[:, dk, 512 * h:512 * h + 512],
-                                         start=(dk == 0), stop=(dk == 3))
-                    nc.vector.scalar_tensor_tensor(
-                        out=F[b][:, cj, 512 * h:512 * h + 512], in0=pq[:],
-                        scalar=k2[b][:, cj:cj + 1], in1=q2b[:, 512 * h:512 * h + 512],
-                        op0=ALU.add, op1=ALU.add)
-                nc.vector.tensor_scalar(out=F[b][:, cj, :], in0=F[b][:, cj, :], scalar1=TINY,
-                                        scalar2=None, op0=ALU.max, op1=ALU.min,
-                                        accum_out=minsq[b][:, cj:cj + 1])
-                nc.scalar.activation(out=F[b][:, cj, :], in_=F[b][:, cj, :], func=ACT.Sqrt)
+        qv = q_proj.rearrange("(p i) d -> p i d", i=8)
+        kv = [k_proj[b].rearrange("(c p j) d -> p c j d", c=2, j=4) for b in range(B)]
+        nc.sync.dma_start(out=q_raw[:, 0:4, :], in_=qv[:, 0:4, :])
+        nc.sync.dma_start(out=k_raw[0][0][:], in_=kv[0][:, 0, :, :])
+        nc.sync.dma_start(out=q_raw[:, 4:8, :], in_=qv[:, 4:8, :])
+        nc.sync.dma_start(out=k_raw[0][1][:], in_=kv[0][:, 1, :, :])
+        nc.sync.dma_start(out=k_raw[1][0], in_=kv[1][:, 0, :, :])
+        nc.sync.dma_start(out=k_raw[1][1], in_=kv[1][:, 1, :, :])
+
+        def norm(src, dst):
+            jn = scr.tile([P, D], BF16, name="jn", tag="jn")
+            nc.scalar.activation(out=jn[:], in_=src, func=ACT.Square, accum_out=dst)
+
+        def q_norm(i):
+            norm(q_raw[:, i, :], q2[:, i:i + 1])
+
+        def k_norm(b, cj):
+            norm(k_raw[b][cj // 4][:, cj % 4, :], k2[b][:, cj:cj + 1])
+
+        def q_tr(i):
+            pt = psum.tile([P, 4, P], BF16, name="pt", tag="tr", bufs=2)
+            for dk in range(4):
+                nc.tensor.transpose(out=pt[:, dk, :], in_=q_raw[:, i, P * dk:P * dk + P],
+                                    identity=ident_bf[:])
+            for s in range(2):
+                nc.vector.tensor_scalar(out=qT[s][:, :, P * i:P * i + P], in0=pt[:, 2 * s:2 * s + 2, :],
+                                        scalar1=-2.0, scalar2=None, op0=ALU.mult)
+
+        def k_tr(b, cj):
+            pt = psum.tile([P, 4, P], BF16, name="pt", tag="tr", bufs=2)
+            for dk in range(4):
+                nc.tensor.transpose(out=pt[:, dk, :],
+                                    in_=k_raw[b][cj // 4][:, cj % 4, P * dk:P * dk + P],
+                                    identity=ident_bf[:])
+            for s in range(2):
+                nc.vector.tensor_copy(out=kT[b][s][:, :, P * cj:P * cj + P], in_=pt[:, 2 * s:2 * s + 2, :])
+
+        def spread_half(vec, dst, hh):
+            pb = psum.tile([P, 512], F32, name="pb", tag="tr", bufs=2)
+            for a in range(4):
+                i = 4 * hh + a
+                nc.tensor.transpose(out=pb[:, P * a:P * a + P],
+                                    in_=vec[:, i:i + 1].to_broadcast([P, P]),
+                                    identity=ident_f[:])
+            nc.scalar.copy(out=dst[:, 512 * hh:512 * hh + 512], in_=pb[:])
+
+        def mm(b, cj, h):
+            pq = psum.tile([P, 512], F32, name="pq", tag="mm", bufs=4)
+            for dk in range(4):
+                nc.tensor.matmul(out=pq[:], lhsT=kT[b][dk // 2][:, dk % 2, P * cj:P * cj + P],
+                                 rhs=qT[dk // 2][:, dk % 2, 512 * h:512 * h + 512],
+                                 start=(dk == 0), stop=(dk == 3))
+            nc.vector.scalar_tensor_tensor(
+                out=F[b][:, cj, 512 * h:512 * h + 512], in0=pq[:],
+                scalar=k2[b][:, cj:cj + 1], in1=q2b[:, 512 * h:512 * h + 512],
+                op0=ALU.add, op1=ALU.add)
+
+        def clamp(b, cj):
+            nc.vector.tensor_scalar(out=F[b][:, cj, :], in0=F[b][:, cj, :], scalar1=TINY,
+                                    scalar2=None, op0=ALU.max, op1=ALU.min,
+                                    accum_out=minsq[b][:, cj:cj + 1])
+
+        def sqrt_(b, cj):
+            nc.scalar.activation(out=F[b][:, cj, :], in_=F[b][:, cj, :], func=ACT.Sqrt)
+
+        def min_sqrt(b):
             nc.scalar.activation(out=mn[b][:], in_=minsq[b][:], func=ACT.Sqrt)
             S[b] = small.tile([P, 8], F32, name="S%d" % b, tag="S%d" % b)
-            for cj in range(8):
-                nc.scalar.activation(out=F[b][:, cj, :], in_=F[b][:, cj, :], func=ACT.Exp,
-                                     bias=mn[b][:, cj:cj + 1], scale=-1.0,
-                                     accum_out=S[b][:, cj:cj + 1])
+
+        def expo(b, cj):
+            nc.scalar.activation(out=F[b][:, cj, :], in_=F[b][:, cj, :], func=ACT.Exp,
+                                 bias=mn[b][:, cj:cj + 1], scale=-1.0,
+                                 accum_out=S[b][:, cj:cj + 1])
+
+        def hilo(b, cj, eng):
+            if eng == "v":
+                nc.vector.tensor_copy(out=TH[b][:, cj, :], in_=F[b][:, cj, :])
+                nc.vector.tensor_tensor(out=TL[b][:, cj, :], in0=F[b][:, cj, :], in1=TH[b][:, cj, :],
+                                        op=ALU.subtract)
+            else:
                 nc.gpsimd.tensor_scalar(out=TH[b][:, cj, :], in0=F[b][:, cj, :], scalar1=1.0,
                                         scalar2=0.0, op0=ALU.mult, op1=ALU.add)
-                lo_eng = nc.vector if cj % 2 == 0 else nc.gpsimd
-                lo_eng.tensor_tensor(out=TL[b][:, cj, :], in0=F[b][:, cj, :],
-                                     in1=TH[b][:, cj, :], op=ALU.subtract)
+                nc.gpsimd.tensor_tensor(out=TL[b][:, cj, :], in0=F[b][:, cj, :], in1=TH[b][:, cj, :],
+                                        op=ALU.subtract)
 
-        phase1(0)
-        k_norms(1)
-        k_transposes(1)
-        phase1(1)
+        def k_flip(b, x, eng):
+            NHL[b][x] = big.tile([P, 2, 8, P], BF16, name="NHL%d%d" % (b, x), tag=NHL_TAGS[b][x],
+                                 align_bytes=64)
+            for s, piece in enumerate((TH[b], TL[b])):
+                pk = psum.tile([P, 8, P], BF16, name="pk", tag="tr", bufs=2)
+                for i in range(8):
+                    nc.tensor.transpose(out=pk[:, i, :], in_=piece[:, x, P * i:P * i + P],
+                                        identity=ident_bf[:])
+                if eng == "v":
+                    nc.vector.tensor_copy(out=NHL[b][x][:, s, :, :], in_=pk[:])
+                else:
+                    nc.scalar.copy(out=NHL[b][x][:, s, :, :], in_=pk[:])
 
-        w_raw = big.tile([P, 4, D], BF16, name="w_raw", tag="sE", align_bytes=64)
+        def split(dst, src):
+            nc.vector.tensor_copy(out=dst[:, :, 0], in_=src[:])
+            nc.vector.tensor_tensor(out=dst[:, :, 1], in0=src[:], in1=dst[:, :, 0], op=ALU.subtract)
+
+        def small_v(b):
+            vcur[b] = small.tile([P, 8], F32, name="v%d" % b, tag="v%d" % b)
+            nc.vector.reciprocal(out=vcur[b][:], in_=S[b][:])
+            vsp[b] = small.tile([P, 8, 2], BF16, name="vsp%d" % b, tag="vsp%d" % b)
+            split(vsp[b], vcur[b])
+
+        def g_mm(b):
+            Rt[b] = psum.tile([P, 8, 2], F32, name="R", tag="mv%d" % b, bufs=1)
+            for i in range(8):
+                idx = 0
+                for cj in range(8):
+                    for piece in (TH[b], TL[b]):
+                        nc.tensor.matmul(out=Rt[b][:, i, :], lhsT=piece[:, cj, P * i:P * i + P],
+                                         rhs=vsp[b][:, cj, :], start=(idx == 0), stop=(idx == 15))
+                        idx += 1
+
+        def r_u_head(b):
+            r = small.tile([P, 8], F32, name="r%d" % b, tag="r%d" % b)
+            nc.vector.tensor_reduce(out=r[:], in_=Rt[b][:], axis=AX.X, op=ALU.add)
+            ucur[b] = small.tile([P, 8], F32, name="u%d" % b, tag="u%d" % b)
+            nc.vector.reciprocal(out=ucur[b][:], in_=r[:])
+            spread_half(ucur[b], ub[b], 0)
+            spread_half(ucur[b], ub[b], 1)
+
+        def r_u_tail(b):
+            usp[b] = small.tile([P, 8, 2], BF16, name="usp%d" % b, tag="usp%d" % b)
+            split(usp[b], ucur[b])
+            Sp[b] = psum.tile([P, XPE, 2], F32, name="Sp", tag="mv%d" % b, bufs=1)
+            for x in range(XPE):
+                idx = 0
+                for i in range(8):
+                    for s in range(2):
+                        nc.tensor.matmul(out=Sp[b][:, x, :], lhsT=NHL[b][x][:, s, i, :],
+                                         rhs=usp[b][:, i, :], start=(idx == 0), stop=(idx == 15))
+                        idx += 1
+
+        def r_u(b, last):
+            r_u_head(b)
+            if not last:
+                r_u_tail(b)
+
+        junk_box = [None]
+
+        def f_stt(b, cj):
+            nc.vector.scalar_tensor_tensor(
+                out=junk_box[0][:], in0=F[b][:, cj, :], scalar=1.0, in1=ub[b][:],
+                op0=ALU.mult, op1=ALU.mult, accum_out=S[b][:, cj:cj + 1])
+
+        for i in range(4):
+            q_norm(i)
+            q_tr(i)
+        for cj in range(4):
+            k_tr(0, cj)
+        spread_half(q2, q2b, 0)
+        for cj in range(4):
+            k_norm(0, cj)
+        mm(0, 0, 0)
+        mm(0, 1, 0)
+        for i in range(4, 8):
+            q_norm(i)
+            q_tr(i)
+        mm(0, 2, 0)
+        mm(0, 3, 0)
+        spread_half(q2, q2b, 1)
+        for cj in range(4, 8):
+            k_tr(0, cj)
+        for cj in range(4):
+            mm(0, cj, 1)
+            clamp(0, cj)
+            sqrt_(0, cj)
+            k_norm(0, 4 + cj)
+        for cj in range(4, 8):
+            mm(0, cj, 0)
+            mm(0, cj, 1)
+            clamp(0, cj)
+            sqrt_(0, cj)
+            k_tr(1, 2 * (cj - 4))
+            k_tr(1, 2 * (cj - 4) + 1)
+            k_norm(1, 2 * (cj - 4))
+            k_norm(1, 2 * (cj - 4) + 1)
+        min_sqrt(0)
+        POOL0 = (0, 2, 4, 6)
+        for cj in range(8):
+            expo(0, cj)
+            mm(1, cj, 0)
+            mm(1, cj, 1)
+            clamp(1, cj)
+            if cj > 0:
+                hilo(0, cj - 1, "g" if cj - 1 in POOL0 else "v")
+        hilo(0, 7, "g" if 7 in POOL0 else "v")
+        small_v(0)
+        for cj in range(8):
+            sqrt_(1, cj)
+        min_sqrt(1)
+        g_mm(0)
+
+        w_raw = big.tile([P, 4, D], BF16, name="w_raw", tag="b0", align_bytes=64)
         nc.sync.dma_start(out=w_raw[:].rearrange("p (u e) c -> p u e c", u=2),
                           in_=w_v.rearrange("(u q e) c -> q u e c", u=2, e=2))
-        wg = big.tile([P, D, 4], BF16, name="wg", tag="sF", align_bytes=64)
-        nc.vector.tensor_copy(out=wg[:], in_=w_raw[:].rearrange("p t c -> p c t"))
+        wg = big.tile([P, D, 4], BF16, name="wg", tag="b1", align_bytes=64)
         wc = const.tile([P, D], U32, name="wc", align_bytes=64)
         ws = const.tile([P, D], U8, name="ws", align_bytes=64)
-        nc.vector.quantize_mx(out=wc[:].bitcast(FP8X4), scales=ws[:],
-                              in_=wg[:].rearrange("p c t -> p (c t)"))
         vpc = [const.tile([P, 2, D], U32, name="vpc%d" % b, align_bytes=64) for b in range(B)]
         vps = [const.tile([P, 2, D], U8, name="vps%d" % b, align_bytes=64) for b in range(B)]
+        v_raw = [None, None]
+        vg = [None, None]
+        vc = [None, None]
+        vs_ = [None, None]
+        vpg = [None, None]
 
-        def value_path(b):
-            v_raw = big.tile([P, 8, D], BF16, name="v_raw", tag=("sA", "sB")[b], align_bytes=64)
-            nc.sync.dma_start(out=v_raw[:].rearrange("p (c j) d -> p c j d", c=2),
+        def v_load(b):
+            v_raw[b] = big.tile([P, 8, D], BF16, name="v_raw", tag=("sA", "sC")[b], align_bytes=64)
+            nc.sync.dma_start(out=v_raw[b][:].rearrange("p (c j) d -> p c j d", c=2),
                               in_=v[b].rearrange("(c p j) d -> p c j d", c=2, j=4))
-            vw = v_raw[:].bitcast(F32)
-            vg = big.tile([P, N, 4], BF16, name="vg", tag="sC", align_bytes=64)
-            vgw = vg[:].bitcast(F32)
+
+        def w_quant():
+            nc.vector.tensor_copy(out=wg[:], in_=w_raw[:].rearrange("p t c -> p c t"))
+            nc.vector.quantize_mx(out=wc[:].bitcast(FP8X4), scales=ws[:],
+                                  in_=wg[:].rearrange("p c t -> p (c t)"))
+
+        def v_tr(b):
+            vw = v_raw[b][:].bitcast(F32)
+            vg[b] = big.tile([P, N, 4], BF16, name="vg", tag=("sC", "sA")[b], align_bytes=64)
+            vgw = vg[b][:].bitcast(F32)
             for g in range(4):
-                pv = psum.tile([P, 2, 2, P], F32, name="pv", tag="tr", bufs=2)
+                pv = psum.tile([P, 2, 2, P], F32, name="pv", tag="mm", bufs=4)
                 for a in range(2):
                     for u in range(2):
                         nc.tensor.transpose(out=pv[:, a, u, :],
@@ -175,11 +305,15 @@ def tile_sinkhornattention_pa_kernel(tc, q_proj, k_proj, v, w_v, out):
                 nc.scalar.copy(
                     out=vgw[:, 256 * g:256 * g + 256, :].rearrange("p (a n) u -> p a n u", a=2),
                     in_=pv[:].rearrange("p a u n -> p a n u"))
-            vc = big.tile([P, N], U32, name="vc", tag="vc", align_bytes=64)
-            vs_ = big.tile([P, N], U8, name="vs_", tag="vs_", align_bytes=64)
-            nc.vector.quantize_mx(out=vc[:].bitcast(FP8X4), scales=vs_[:],
-                                  in_=vg[:].rearrange("p n t -> p (n t)"))
-            vpg = big.tile([P, 2, D, 4], BF16, name="vpg", tag="sD", align_bytes=64)
+
+        def v_quant(b):
+            vc[b] = big.tile([P, N], U32, name="vc", tag="vc", align_bytes=64)
+            vs_[b] = big.tile([P, N], U8, name="vs_", tag="vs_", align_bytes=64)
+            nc.vector.quantize_mx(out=vc[b][:].bitcast(FP8X4), scales=vs_[b][:],
+                                  in_=vg[b][:].rearrange("p n t -> p (n t)"))
+
+        def vp_mx(b):
+            vpg[b] = big.tile([P, 2, D, 4], BF16, name="vpg", tag=("sA", "sC")[b], align_bytes=64)
             for c in range(2):
                 for eq in range(4):
                     pvp = psum.tile([P, 4, P], F32, name="pvp", tag="mm", bufs=4)
@@ -187,87 +321,130 @@ def tile_sinkhornattention_pa_kernel(tc, q_proj, k_proj, v, w_v, out):
                         cj = 4 * c + j
                         nc.tensor.matmul_mx(
                             out=pvp[:, j, :],
-                            lhsT=vc[:, P * cj:P * cj + P].bitcast(FP8X4),
-                            lhsT_scale=vs_[:, P * cj:P * cj + P],
+                            lhsT=vc[b][:, P * cj:P * cj + P].bitcast(FP8X4),
+                            lhsT_scale=vs_[b][:, P * cj:P * cj + P],
                             rhs=wc[:, P * eq:P * eq + P].bitcast(FP8X4),
                             rhs_scale=ws[:, P * eq:P * eq + P],
                             start=True, stop=True)
-                    nc.scalar.copy(out=vpg[:, c, P * eq:P * eq + P, :],
+                    nc.scalar.copy(out=vpg[b][:, c, P * eq:P * eq + P, :],
                                    in_=pvp[:].rearrange("p j e -> p e j"))
+
+        def vp_quant(b):
             nc.vector.quantize_mx(out=vpc[b][:].rearrange("p c e -> p (c e)").bitcast(FP8X4),
                                   scales=vps[b][:].rearrange("p c e -> p (c e)"),
-                                  in_=vpg[:].rearrange("p c e j -> p (c e j)"))
+                                  in_=vpg[b][:].rearrange("p c e j -> p (c e j)"))
 
-        junk = big.tile([P, T], F32, name="junk", tag="sG", align_bytes=64)
-        ub = [big.tile([P, T], F32, name="ub%d" % b, tag="ub%d" % b) for b in range(B)]
-        vcur = [None, None]
-        for it in range(ITERS):
-            vsp = [None, None]
-            for b in range(B):
-                with tc.high_priority():
-                    vcur[b] = small.tile([P, 8], F32, name="v%d" % b, tag="v%d" % b)
-                    nc.vector.reciprocal(out=vcur[b][:], in_=S[b][:])
-                    vsp[b] = small.tile([P, 8, 2], BF16, name="vsp%d" % b, tag="vsp%d" % b)
-                    nc.vector.tensor_copy(out=vsp[b][:, :, 0], in_=vcur[b][:])
-                    nc.vector.tensor_tensor(out=vsp[b][:, :, 1], in0=vcur[b][:],
-                                            in1=vsp[b][:, :, 0], op=ALU.subtract)
-                    R = psum.tile([P, 8, 2], F32, name="R", tag="mv", bufs=2)
-                    for i in range(8):
-                        idx = 0
-                        for cj in range(8):
-                            for piece in (TH[b], TL[b]):
-                                nc.tensor.matmul(out=R[:, i, :],
-                                                 lhsT=piece[:, cj, P * i:P * i + P],
-                                                 rhs=vsp[b][:, cj, :],
-                                                 start=(idx == 0), stop=(idx == 15))
-                                idx += 1
-                    r = small.tile([P, 8], F32, name="r%d" % b, tag="r%d" % b)
-                    nc.vector.tensor_reduce(out=r[:], in_=R[:], axis=AX.X, op=ALU.add)
-                    u = small.tile([P, 8], F32, name="u%d" % b, tag="u%d" % b)
-                    nc.vector.reciprocal(out=u[:], in_=r[:])
-                    spread(u, ub[b])
-                if it == ITERS - 1:
-                    for cj in range(8):
-                        nc.scalar.activation(out=F[b][:, cj, :], in_=F[b][:, cj, :], func=ACT.Copy,
-                                             scale=vcur[b][:, cj:cj + 1])
-            if it < ITERS - 1:
-                for b in range(B):
-                    S[b] = small.tile([P, 8], F32, name="S%d" % b, tag="S%d" % b)
-                    for cj in range(8):
-                        nc.vector.scalar_tensor_tensor(
-                            out=junk[:], in0=F[b][:, cj, :], scalar=1.0, in1=ub[b][:],
-                            op0=ALU.mult, op1=ALU.mult, accum_out=S[b][:, cj:cj + 1])
+        v_load(0)
 
-        value_path(0)
-        value_path(1)
+        junk_box[0] = big.tile([P, T], F32, name="junk", tag="sG", align_bytes=64)
+        NV = 8 - XPE
+        RU_AT = 4
+        POOL1 = (0, 3, 6)
 
-        for b in range(B):
-            pig = big.tile([P, 2, T, 4], BF16, name="pig%d" % b, tag="th%d" % b, align_bytes=64)
-            pic = big.tile([P, 2, T], U32, name="pic%d" % b, tag="tl%d" % b, align_bytes=64)
-            pis = const.tile([P, 2, T], U8, name="pis%d" % b, align_bytes=64)
+        def w_scale(b):
+            for cj in range(8):
+                if cj % 2 == 0:
+                    nc.scalar.activation(out=F[b][:, cj, :], in_=F[b][:, cj, :], func=ACT.Copy,
+                                         scale=vcur[b][:, cj:cj + 1])
+                else:
+                    nc.gpsimd.tensor_scalar(out=F[b][:, cj, :], in0=F[b][:, cj, :],
+                                            scalar1=vcur[b][:, cj:cj + 1], scalar2=0.0,
+                                            op0=ALU.mult, op1=ALU.add)
+
+        def f_begin(b):
+            S[b] = small.tile([P, 8], F32, name="S%d" % b, tag="S%d" % b)
+
+        def f_end(b):
+            nc.vector.tensor_reduce(out=S[b][:, 0:XPE], in_=Sp[b][:], axis=AX.X, op=ALU.add)
+            small_v(b)
+            g_mm(b)
+
+        expo(1, 0)
+        r_u_head(0)
+        for x in range(XPE):
+            k_flip(0, x, "v")
+        r_u_tail(0)
+        for cj in range(8):
+            if cj > 0:
+                expo(1, cj)
+            hilo(1, cj, "g" if cj in POOL1 else "v")
+        for x in range(XPE):
+            k_flip(1, x, "s")
+        small_v(1)
+        g_mm(1)
+
+        pig = [None, None]
+        pic = [None, None]
+        pis = [const.tile([P, 2, T], U8, name="pis%d" % b, align_bytes=64) for b in range(B)]
+
+        def pi_half(b, h, between):
+            sl = slice(512 * h, 512 * h + 512)
+            for c in range(2):
+                nc.vector.tensor_tensor(
+                    out=pig[b][:, c, sl, :],
+                    in0=F[b][:, 4 * c:4 * c + 4, sl].rearrange("p j t -> p t j"),
+                    in1=ub[b][:, sl].unsqueeze(2).to_broadcast([P, 512, 4]),
+                    op=ALU.mult)
+                if c == 0 and between is not None:
+                    r_u(between[0], between[1])
+            for c in range(2):
+                nc.vector.quantize_mx(out=pic[b][:, c, sl].bitcast(FP8X4), scales=pis[b][:, c, sl],
+                                      in_=pig[b][:, c, sl, :].rearrange("p t j -> p (t j)"))
+
+        def out_half(b, h):
             ov = out[b].rearrange("(p i) d -> p i d", i=8)
-            for h in range(2):
-                sl = slice(512 * h, 512 * h + 512)
+            ost = big.tile([P, 4, D], F32, name="ost", tag=("sA", "sC")[h], align_bytes=64)
+            for a in range(4):
+                i = 4 * h + a
+                po = psum.tile([P, D], F32, name="po", tag="mm", bufs=4)
                 for c in range(2):
-                    nc.vector.tensor_tensor(
-                        out=pig[:, c, sl, :],
-                        in0=F[b][:, 4 * c:4 * c + 4, sl].rearrange("p j t -> p t j"),
-                        in1=ub[b][:, sl].unsqueeze(2).to_broadcast([P, 512, 4]),
-                        op=ALU.mult)
-                for c in range(2):
-                    nc.vector.quantize_mx(out=pic[:, c, sl].bitcast(FP8X4), scales=pis[:, c, sl],
-                                          in_=pig[:, c, sl, :].rearrange("p t j -> p (t j)"))
-                ost = big.tile([P, 4, D], F32, name="ost", tag=("sA", "sB")[h], align_bytes=64)
-                for a in range(4):
-                    i = 4 * h + a
-                    po = psum.tile([P, D], F32, name="po", tag="mm", bufs=4)
-                    for c in range(2):
-                        nc.tensor.matmul_mx(
-                            out=po[:],
-                            lhsT=pic[:, c, P * i:P * i + P].bitcast(FP8X4),
-                            lhsT_scale=pis[:, c, P * i:P * i + P],
-                            rhs=vpc[b][:, c, :].bitcast(FP8X4),
-                            rhs_scale=vps[b][:, c, :],
-                            start=(c == 0), stop=(c == 1))
-                    nc.scalar.copy(out=ost[:, a, :], in_=po[:])
-                nc.sync.dma_start(out=ov[:, 4 * h:4 * h + 4, :], in_=ost[:])
+                    nc.tensor.matmul_mx(
+                        out=po[:],
+                        lhsT=pic[b][:, c, P * i:P * i + P].bitcast(FP8X4),
+                        lhsT_scale=pis[b][:, c, P * i:P * i + P],
+                        rhs=vpc[b][:, c, :].bitcast(FP8X4),
+                        rhs_scale=vps[b][:, c, :],
+                        start=(c == 0), stop=(c == 1))
+                nc.scalar.copy(out=ost[:, a, :], in_=po[:])
+            nc.sync.dma_start(out=ov[:, 4 * h:4 * h + 4, :], in_=ost[:])
+
+        extra = {
+            0: lambda: (w_quant(), v_tr(0)),
+            1: lambda: v_quant(0),
+            2: lambda: (vp_mx(0), v_load(1)),
+            3: lambda: (vp_quant(0), v_tr(1)),
+            4: lambda: (v_quant(1), vp_mx(1)),
+            5: lambda: vp_quant(1),
+        }
+        runs = [
+            ("f", 0, 0, (1, False)),
+            ("f", 1, 0, (0, False)),
+            ("f", 0, 1, (1, False)),
+            ("f", 1, 1, (0, False)),
+            ("f", 0, 2, (1, False)),
+            ("f", 1, 2, (0, False)),
+            ("f", 0, 3, (1, False)),
+            ("f", 1, 3, (0, True)),
+            ("pi", 0, 0, (1, True)),
+            ("pi", 0, 1, None),
+            ("pi", 1, 0, None),
+            ("pi", 1, 1, None),
+        ]
+        for n_run, (kind, b, idx, between) in enumerate(runs):
+            if kind == "f":
+                f_begin(b)
+                for k in range(NV):
+                    f_stt(b, XPE + k)
+                    if k == RU_AT - 1 and between is not None:
+                        r_u(between[0], between[1])
+                f_end(b)
+                if idx == ITERS - 2:
+                    w_scale(b)
+            else:
+                if idx == 0:
+                    pig[b] = big.tile([P, 2, T, 4], BF16, name="pig%d" % b, tag="th%d" % b, align_bytes=64)
+                    pic[b] = big.tile([P, 2, T], U32, name="pic%d" % b, tag="tl%d" % b, align_bytes=64)
+                pi_half(b, idx, between)
+                out_half(b, idx)
+            if n_run in extra:
+                extra[n_run]()

@@ -61,6 +61,9 @@ def tile_sinkhornattention_pa_kernel(tc, q_proj, k_proj, v, w_v, out):
         ub = [big.tile([P, T], F32, name="ub%d" % b, tag="ub%d" % b) for b in range(B)]
         NHL = [[None] * XPE, [None] * XPE]
         NHL_TAGS = (("e0", "e1", "d0"), ("d1", "f0", "f1"))
+        wc = const.tile([P, D], U32, name="wc", align_bytes=64)
+        ws = const.tile([P, D], U8, name="ws", align_bytes=64)
+        idle_bank = psum.tile([P, D], F32, name="idle_bank", tag="idle", bufs=1)
         S = [None, None]
         vcur = [None, None]
         vsp = [None, None]
@@ -116,7 +119,7 @@ def tile_sinkhornattention_pa_kernel(tc, q_proj, k_proj, v, w_v, out):
             nc.scalar.copy(out=dst[:, 512 * hh:512 * hh + 512], in_=pb[:])
 
         def mm(b, cj, h):
-            pq = psum.tile([P, 512], F32, name="pq", tag="mm", bufs=4)
+            pq = psum.tile([P, 512], F32, name="pq", tag="mm", bufs=3)
             for dk in range(4):
                 nc.tensor.matmul(out=pq[:], lhsT=kT[b][dk // 2][:, dk % 2, P * cj:P * cj + P],
                                  rhs=qT[dk // 2][:, dk % 2, 512 * h:512 * h + 512],
@@ -177,9 +180,15 @@ def tile_sinkhornattention_pa_kernel(tc, q_proj, k_proj, v, w_v, out):
             vsp[b] = small.tile([P, 8, 2], BF16, name="vsp%d" % b, tag="vsp%d" % b)
             split(vsp[b], vcur[b])
 
+        def keep_clock():
+            nc.tensor.matmul_mx(out=idle_bank[:], lhsT=wc[:, 0:P].bitcast(FP8X4), lhsT_scale=ws[:, 0:P],
+                                rhs=wc[:].bitcast(FP8X4), rhs_scale=ws[:], start=True, stop=True)
+
         def g_mm(b):
             Rt[b] = psum.tile([P, 8, 2], F32, name="R", tag="mv%d" % b, bufs=1)
             for i in range(8):
+                if i % 2 == 0:
+                    keep_clock()
                 idx = 0
                 for cj in range(8):
                     for piece in (TH[b], TL[b]):
@@ -200,6 +209,8 @@ def tile_sinkhornattention_pa_kernel(tc, q_proj, k_proj, v, w_v, out):
             split(usp[b], ucur[b])
             Sp[b] = psum.tile([P, XPE, 2], F32, name="Sp", tag="mv%d" % b, bufs=1)
             for x in range(XPE):
+                if x % 2 == 0:
+                    keep_clock()
                 idx = 0
                 for i in range(8):
                     for s in range(2):
@@ -265,14 +276,15 @@ def tile_sinkhornattention_pa_kernel(tc, q_proj, k_proj, v, w_v, out):
         for cj in range(8):
             sqrt_(1, cj)
         min_sqrt(1)
-        g_mm(0)
-
         w_raw = big.tile([P, 4, D], BF16, name="w_raw", tag="b0", align_bytes=64)
         nc.sync.dma_start(out=w_raw[:].rearrange("p (u e) c -> p u e c", u=2),
                           in_=w_v.rearrange("(u q e) c -> q u e c", u=2, e=2))
         wg = big.tile([P, D, 4], BF16, name="wg", tag="b1", align_bytes=64)
-        wc = const.tile([P, D], U32, name="wc", align_bytes=64)
-        ws = const.tile([P, D], U8, name="ws", align_bytes=64)
+        nc.vector.tensor_copy(out=wg[:], in_=w_raw[:].rearrange("p t c -> p c t"))
+        nc.vector.quantize_mx(out=wc[:].bitcast(FP8X4), scales=ws[:],
+                              in_=wg[:].rearrange("p c t -> p (c t)"))
+        g_mm(0)
+
         vpc = [const.tile([P, 2, D], U32, name="vpc%d" % b, align_bytes=64) for b in range(B)]
         vps = [const.tile([P, 2, D], U8, name="vps%d" % b, align_bytes=64) for b in range(B)]
         v_raw = [None, None]
@@ -286,17 +298,12 @@ def tile_sinkhornattention_pa_kernel(tc, q_proj, k_proj, v, w_v, out):
             nc.sync.dma_start(out=v_raw[b][:].rearrange("p (c j) d -> p c j d", c=2),
                               in_=v[b].rearrange("(c p j) d -> p c j d", c=2, j=4))
 
-        def w_quant():
-            nc.vector.tensor_copy(out=wg[:], in_=w_raw[:].rearrange("p t c -> p c t"))
-            nc.vector.quantize_mx(out=wc[:].bitcast(FP8X4), scales=ws[:],
-                                  in_=wg[:].rearrange("p c t -> p (c t)"))
-
         def v_tr(b):
             vw = v_raw[b][:].bitcast(F32)
             vg[b] = big.tile([P, N, 4], BF16, name="vg", tag=("sC", "sA")[b], align_bytes=64)
             vgw = vg[b][:].bitcast(F32)
             for g in range(4):
-                pv = psum.tile([P, 2, 2, P], F32, name="pv", tag="mm", bufs=4)
+                pv = psum.tile([P, 2, 2, P], F32, name="pv", tag="mm", bufs=3)
                 for a in range(2):
                     for u in range(2):
                         nc.tensor.transpose(out=pv[:, a, u, :],
@@ -316,7 +323,7 @@ def tile_sinkhornattention_pa_kernel(tc, q_proj, k_proj, v, w_v, out):
             vpg[b] = big.tile([P, 2, D, 4], BF16, name="vpg", tag=("sA", "sC")[b], align_bytes=64)
             for c in range(2):
                 for eq in range(4):
-                    pvp = psum.tile([P, 4, P], F32, name="pvp", tag="mm", bufs=4)
+                    pvp = psum.tile([P, 4, P], F32, name="pvp", tag="mm", bufs=3)
                     for j in range(4):
                         cj = 4 * c + j
                         nc.tensor.matmul_mx(
@@ -396,7 +403,7 @@ def tile_sinkhornattention_pa_kernel(tc, q_proj, k_proj, v, w_v, out):
             ost = big.tile([P, 4, D], F32, name="ost", tag=("sA", "sC")[h], align_bytes=64)
             for a in range(4):
                 i = 4 * h + a
-                po = psum.tile([P, D], F32, name="po", tag="mm", bufs=4)
+                po = psum.tile([P, D], F32, name="po", tag="mm", bufs=3)
                 for c in range(2):
                     nc.tensor.matmul_mx(
                         out=po[:],
@@ -409,7 +416,7 @@ def tile_sinkhornattention_pa_kernel(tc, q_proj, k_proj, v, w_v, out):
             nc.sync.dma_start(out=ov[:, 4 * h:4 * h + 4, :], in_=ost[:])
 
         extra = {
-            0: lambda: (w_quant(), v_tr(0)),
+            0: lambda: v_tr(0),
             1: lambda: v_quant(0),
             2: lambda: (vp_mx(0), v_load(1)),
             3: lambda: (vp_quant(0), v_tr(1)),

@@ -21,7 +21,7 @@ ITERS = 5
 TINY = 2.0 ** -100
 FLOPS = 2 * B * T * N * D + 2 * B * N * D * D + 2 * B * T * N * D
 
-XPE = 3
+RU_AT = 7
 
 
 def tile_sinkhornattention_pa_kernel(tc, q_proj, k_proj, v, w_v, out):
@@ -40,16 +40,12 @@ def tile_sinkhornattention_pa_kernel(tc, q_proj, k_proj, v, w_v, out):
         make_identity(nc, ident_f[:])
 
         q_raw = big.tile([P, 8, D], BF16, name="q_raw", tag="sA", align_bytes=64)
-        k_raw = [
-            [big.tile([P, 4, D], BF16, name="k_raw0%d" % c, tag="b%d" % c, align_bytes=64) for c in range(2)],
-        ]
-        k_raw1 = big.tile([P, 8, D], BF16, name="k_raw1", tag="sC", align_bytes=64)
-        k_raw.append([k_raw1[:, 0:4, :], k_raw1[:, 4:8, :]])
-        qT = [big.tile([P, 2, T], BF16, name="qT%d" % s, tag="d%d" % s, align_bytes=64) for s in range(2)]
-        kT = [
-            [big.tile([P, 2, N], BF16, name="kT0%d" % s, tag="e%d" % s, align_bytes=64) for s in range(2)],
-            [big.tile([P, 2, N], BF16, name="kT1%d" % s, tag="f%d" % s, align_bytes=64) for s in range(2)],
-        ]
+        k_raw = [big.tile([P, 8, D], BF16, name="k_raw%d" % b, tag=("sB", "sC")[b], align_bytes=64)
+                 for b in range(B)]
+        v_raw = [None, None]
+        qT = big.tile([P, 4, T], BF16, name="qT", tag="sD", align_bytes=64)
+        kT = [big.tile([P, 4, N], BF16, name="kT%d" % b, tag=("sE", "sF")[b], align_bytes=64)
+              for b in range(B)]
         q2 = const.tile([P, 8], F32, name="q2")
         k2 = [const.tile([P, 8], F32, name="k2_%d" % b) for b in range(B)]
         q2b = big.tile([P, T], F32, name="q2b", tag="sG", align_bytes=64)
@@ -59,27 +55,19 @@ def tile_sinkhornattention_pa_kernel(tc, q_proj, k_proj, v, w_v, out):
         minsq = [const.tile([P, 8], F32, name="minsq%d" % b) for b in range(B)]
         mn = [const.tile([P, 8], F32, name="mn%d" % b) for b in range(B)]
         ub = [big.tile([P, T], F32, name="ub%d" % b, tag="ub%d" % b) for b in range(B)]
-        NHL = [[None] * XPE, [None] * XPE]
-        NHL_TAGS = (("e0", "e1", "d0"), ("d1", "f0", "f1"))
-        wc = const.tile([P, D], U32, name="wc", align_bytes=64)
-        ws = const.tile([P, D], U8, name="ws", align_bytes=64)
-        idle_bank = psum.tile([P, D], F32, name="idle_bank", tag="idle", bufs=1)
-        S = [None, None]
+        sums = [None, None]
         vcur = [None, None]
         vsp = [None, None]
-        usp = [None, None]
         Rt = [None, None]
-        Sp = [None, None]
-        ucur = [None, None]
 
         qv = q_proj.rearrange("(p i) d -> p i d", i=8)
         kv = [k_proj[b].rearrange("(c p j) d -> p c j d", c=2, j=4) for b in range(B)]
         nc.sync.dma_start(out=q_raw[:, 0:4, :], in_=qv[:, 0:4, :])
-        nc.sync.dma_start(out=k_raw[0][0][:], in_=kv[0][:, 0, :, :])
+        nc.sync.dma_start(out=k_raw[0][:, 0:4, :], in_=kv[0][:, 0, :, :])
         nc.sync.dma_start(out=q_raw[:, 4:8, :], in_=qv[:, 4:8, :])
-        nc.sync.dma_start(out=k_raw[0][1][:], in_=kv[0][:, 1, :, :])
-        nc.sync.dma_start(out=k_raw[1][0], in_=kv[1][:, 0, :, :])
-        nc.sync.dma_start(out=k_raw[1][1], in_=kv[1][:, 1, :, :])
+        nc.sync.dma_start(out=k_raw[0][:, 4:8, :], in_=kv[0][:, 1, :, :])
+        nc.sync.dma_start(out=k_raw[1][:, 0:4, :], in_=kv[1][:, 0, :, :])
+        nc.sync.dma_start(out=k_raw[1][:, 4:8, :], in_=kv[1][:, 1, :, :])
 
         def norm(src, dst):
             jn = scr.tile([P, D], BF16, name="jn", tag="jn")
@@ -89,25 +77,22 @@ def tile_sinkhornattention_pa_kernel(tc, q_proj, k_proj, v, w_v, out):
             norm(q_raw[:, i, :], q2[:, i:i + 1])
 
         def k_norm(b, cj):
-            norm(k_raw[b][cj // 4][:, cj % 4, :], k2[b][:, cj:cj + 1])
+            norm(k_raw[b][:, cj, :], k2[b][:, cj:cj + 1])
 
         def q_tr(i):
             pt = psum.tile([P, 4, P], BF16, name="pt", tag="tr", bufs=2)
             for dk in range(4):
                 nc.tensor.transpose(out=pt[:, dk, :], in_=q_raw[:, i, P * dk:P * dk + P],
                                     identity=ident_bf[:])
-            for s in range(2):
-                nc.vector.tensor_scalar(out=qT[s][:, :, P * i:P * i + P], in0=pt[:, 2 * s:2 * s + 2, :],
-                                        scalar1=-2.0, scalar2=None, op0=ALU.mult)
+            nc.vector.tensor_scalar(out=qT[:, :, P * i:P * i + P], in0=pt[:], scalar1=-2.0,
+                                    scalar2=None, op0=ALU.mult)
 
         def k_tr(b, cj):
             pt = psum.tile([P, 4, P], BF16, name="pt", tag="tr", bufs=2)
             for dk in range(4):
-                nc.tensor.transpose(out=pt[:, dk, :],
-                                    in_=k_raw[b][cj // 4][:, cj % 4, P * dk:P * dk + P],
+                nc.tensor.transpose(out=pt[:, dk, :], in_=k_raw[b][:, cj, P * dk:P * dk + P],
                                     identity=ident_bf[:])
-            for s in range(2):
-                nc.vector.tensor_copy(out=kT[b][s][:, :, P * cj:P * cj + P], in_=pt[:, 2 * s:2 * s + 2, :])
+            nc.vector.tensor_copy(out=kT[b][:, :, P * cj:P * cj + P], in_=pt[:])
 
         def spread_half(vec, dst, hh):
             pb = psum.tile([P, 512], F32, name="pb", tag="tr", bufs=2)
@@ -119,10 +104,10 @@ def tile_sinkhornattention_pa_kernel(tc, q_proj, k_proj, v, w_v, out):
             nc.scalar.copy(out=dst[:, 512 * hh:512 * hh + 512], in_=pb[:])
 
         def mm(b, cj, h):
-            pq = psum.tile([P, 512], F32, name="pq", tag="mm", bufs=3)
+            pq = psum.tile([P, 512], F32, name="pq", tag="ring", bufs=4)
             for dk in range(4):
-                nc.tensor.matmul(out=pq[:], lhsT=kT[b][dk // 2][:, dk % 2, P * cj:P * cj + P],
-                                 rhs=qT[dk // 2][:, dk % 2, 512 * h:512 * h + 512],
+                nc.tensor.matmul(out=pq[:], lhsT=kT[b][:, dk, P * cj:P * cj + P],
+                                 rhs=qT[:, dk, 512 * h:512 * h + 512],
                                  start=(dk == 0), stop=(dk == 3))
             nc.vector.scalar_tensor_tensor(
                 out=F[b][:, cj, 512 * h:512 * h + 512], in0=pq[:],
@@ -139,15 +124,15 @@ def tile_sinkhornattention_pa_kernel(tc, q_proj, k_proj, v, w_v, out):
 
         def min_sqrt(b):
             nc.scalar.activation(out=mn[b][:], in_=minsq[b][:], func=ACT.Sqrt)
-            S[b] = small.tile([P, 8], F32, name="S%d" % b, tag="S%d" % b)
+            sums[b] = small.tile([P, 8], F32, name="sums%d" % b, tag="sums%d" % b)
 
         def expo(b, cj):
             nc.scalar.activation(out=F[b][:, cj, :], in_=F[b][:, cj, :], func=ACT.Exp,
                                  bias=mn[b][:, cj:cj + 1], scale=-1.0,
-                                 accum_out=S[b][:, cj:cj + 1])
+                                 accum_out=sums[b][:, cj:cj + 1])
 
-        def hilo(b, cj, eng):
-            if eng == "v":
+        def hilo(b, cj, on_vector):
+            if on_vector:
                 nc.vector.tensor_copy(out=TH[b][:, cj, :], in_=F[b][:, cj, :])
                 nc.vector.tensor_tensor(out=TL[b][:, cj, :], in0=F[b][:, cj, :], in1=TH[b][:, cj, :],
                                         op=ALU.subtract)
@@ -157,78 +142,102 @@ def tile_sinkhornattention_pa_kernel(tc, q_proj, k_proj, v, w_v, out):
                 nc.gpsimd.tensor_tensor(out=TL[b][:, cj, :], in0=F[b][:, cj, :], in1=TH[b][:, cj, :],
                                         op=ALU.subtract)
 
-        def k_flip(b, x, eng):
-            NHL[b][x] = big.tile([P, 2, 8, P], BF16, name="NHL%d%d" % (b, x), tag=NHL_TAGS[b][x],
-                                 align_bytes=64)
-            for s, piece in enumerate((TH[b], TL[b])):
-                pk = psum.tile([P, 8, P], BF16, name="pk", tag="tr", bufs=2)
-                for i in range(8):
-                    nc.tensor.transpose(out=pk[:, i, :], in_=piece[:, x, P * i:P * i + P],
-                                        identity=ident_bf[:])
-                if eng == "v":
-                    nc.vector.tensor_copy(out=NHL[b][x][:, s, :, :], in_=pk[:])
-                else:
-                    nc.scalar.copy(out=NHL[b][x][:, s, :, :], in_=pk[:])
-
-        def split(dst, src):
-            nc.vector.tensor_copy(out=dst[:, :, 0], in_=src[:])
-            nc.vector.tensor_tensor(out=dst[:, :, 1], in0=src[:], in1=dst[:, :, 0], op=ALU.subtract)
-
-        def small_v(b):
+        def g_update(b):
             vcur[b] = small.tile([P, 8], F32, name="v%d" % b, tag="v%d" % b)
-            nc.vector.reciprocal(out=vcur[b][:], in_=S[b][:])
+            nc.vector.reciprocal(out=vcur[b][:], in_=sums[b][:])
             vsp[b] = small.tile([P, 8, 2], BF16, name="vsp%d" % b, tag="vsp%d" % b)
-            split(vsp[b], vcur[b])
-
-        def keep_clock():
-            nc.tensor.matmul_mx(out=idle_bank[:], lhsT=wc[:, 0:P].bitcast(FP8X4), lhsT_scale=ws[:, 0:P],
-                                rhs=wc[:].bitcast(FP8X4), rhs_scale=ws[:], start=True, stop=True)
-
-        def g_mm(b):
+            nc.vector.tensor_copy(out=vsp[b][:, :, 0], in_=vcur[b][:])
+            nc.vector.tensor_tensor(out=vsp[b][:, :, 1], in0=vcur[b][:], in1=vsp[b][:, :, 0],
+                                    op=ALU.subtract)
             Rt[b] = psum.tile([P, 8, 2], F32, name="R", tag="mv%d" % b, bufs=1)
             for i in range(8):
-                if i % 2 == 0:
-                    keep_clock()
-                idx = 0
                 for cj in range(8):
-                    for piece in (TH[b], TL[b]):
+                    for s, piece in enumerate((TH[b], TL[b])):
                         nc.tensor.matmul(out=Rt[b][:, i, :], lhsT=piece[:, cj, P * i:P * i + P],
-                                         rhs=vsp[b][:, cj, :], start=(idx == 0), stop=(idx == 15))
-                        idx += 1
+                                         rhs=vsp[b][:, cj, :],
+                                         start=(cj == 0 and s == 0), stop=(cj == 7 and s == 1))
 
-        def r_u_head(b):
+        def u_of(b):
             r = small.tile([P, 8], F32, name="r%d" % b, tag="r%d" % b)
             nc.vector.tensor_reduce(out=r[:], in_=Rt[b][:], axis=AX.X, op=ALU.add)
-            ucur[b] = small.tile([P, 8], F32, name="u%d" % b, tag="u%d" % b)
-            nc.vector.reciprocal(out=ucur[b][:], in_=r[:])
-            spread_half(ucur[b], ub[b], 0)
-            spread_half(ucur[b], ub[b], 1)
+            u = small.tile([P, 8], F32, name="u%d" % b, tag="u%d" % b)
+            nc.vector.reciprocal(out=u[:], in_=r[:])
+            for hh in range(2):
+                spread_half(u, ub[b], hh)
 
-        def r_u_tail(b):
-            usp[b] = small.tile([P, 8, 2], BF16, name="usp%d" % b, tag="usp%d" % b)
-            split(usp[b], ucur[b])
-            Sp[b] = psum.tile([P, XPE, 2], F32, name="Sp", tag="mv%d" % b, bufs=1)
-            for x in range(XPE):
-                if x % 2 == 0:
-                    keep_clock()
-                idx = 0
-                for i in range(8):
-                    for s in range(2):
-                        nc.tensor.matmul(out=Sp[b][:, x, :], lhsT=NHL[b][x][:, s, i, :],
-                                         rhs=usp[b][:, i, :], start=(idx == 0), stop=(idx == 15))
-                        idx += 1
+        def f_update(b, step):
+            sums[b] = small.tile([P, 8], F32, name="sums%d" % b, tag="sums%d" % b)
+            for cj in range(8):
+                if cj == RU_AT:
+                    u_of(1 - b)
+                    vp_eighth(step)
+                nc.vector.scalar_tensor_tensor(
+                    out=junk[:], in0=F[b][:, cj, :], scalar=1.0, in1=ub[b][:],
+                    op0=ALU.mult, op1=ALU.mult, accum_out=sums[b][:, cj:cj + 1])
 
-        def r_u(b, last):
-            r_u_head(b)
-            if not last:
-                r_u_tail(b)
+        wc = const.tile([P, D], U32, name="wc", align_bytes=64)
+        ws = const.tile([P, D], U8, name="ws", align_bytes=64)
+        vpc = [const.tile([P, 2, D], U32, name="vpc%d" % b, align_bytes=64) for b in range(B)]
+        vps = [const.tile([P, 2, D], U8, name="vps%d" % b, align_bytes=64) for b in range(B)]
+        vg = [None, None]
+        vc = [None, None]
+        vs_ = [None, None]
+        vpg = [None, None]
 
-        junk_box = [None]
+        def v_load(b):
+            v_raw[b] = big.tile([P, 8, D], BF16, name="v_raw%d" % b, tag=("sA", "sD")[b], align_bytes=64)
+            nc.sync.dma_start(out=v_raw[b][:].rearrange("p (c j) d -> p c j d", c=2),
+                              in_=v[b].rearrange("(c p j) d -> p c j d", c=2, j=4))
 
-        def f_stt(b, cj):
-            nc.vector.scalar_tensor_tensor(
-                out=junk_box[0][:], in0=F[b][:, cj, :], scalar=1.0, in1=ub[b][:],
-                op0=ALU.mult, op1=ALU.mult, accum_out=S[b][:, cj:cj + 1])
+        def w_quant():
+            nc.vector.tensor_copy(out=wg[:], in_=w_raw[:].rearrange("p t c -> p c t"))
+            nc.vector.quantize_mx(out=wc[:].bitcast(FP8X4), scales=ws[:],
+                                  in_=wg[:].rearrange("p c t -> p (c t)"))
+
+        def v_tr(b):
+            vw = v_raw[b][:].bitcast(F32)
+            vg[b] = big.tile([P, N, 4], BF16, name="vg", tag=("sB", "sC")[b], align_bytes=64)
+            vgw = vg[b][:].bitcast(F32)
+            for g in range(4):
+                pv = psum.tile([P, 2, 2, P], F32, name="pv", tag="ring", bufs=4)
+                for a in range(2):
+                    for u in range(2):
+                        nc.tensor.transpose(out=pv[:, a, u, :],
+                                            in_=vw[:, 2 * g + a, P * u:P * u + P],
+                                            identity=ident_f[:])
+                nc.vector.tensor_copy(
+                    out=vgw[:, 256 * g:256 * g + 256, :].rearrange("p (a n) u -> p a n u", a=2),
+                    in_=pv[:].rearrange("p a u n -> p a n u"))
+
+        def v_quant(b):
+            vc[b] = big.tile([P, N], U32, name="vc", tag="vc%d" % b, align_bytes=64)
+            vs_[b] = big.tile([P, N], U8, name="vs_", tag="vs_%d" % b, align_bytes=64)
+            nc.vector.quantize_mx(out=vc[b][:].bitcast(FP8X4), scales=vs_[b][:],
+                                  in_=vg[b][:].rearrange("p n t -> p (n t)"))
+
+        def vp_eighth(step):
+            b = step // 4
+            c = (step % 4) // 2
+            if step % 4 == 0:
+                vpg[b] = big.tile([P, 2, D, 4], BF16, name="vpg", tag=("sE", "sF")[b], align_bytes=64)
+            for eq in (2 * (step % 2), 2 * (step % 2) + 1):
+                pvp = psum.tile([P, 4, P], F32, name="pvp", tag="ring", bufs=4)
+                for j in range(4):
+                    cj = 4 * c + j
+                    nc.tensor.matmul_mx(
+                        out=pvp[:, j, :],
+                        lhsT=vc[b][:, P * cj:P * cj + P].bitcast(FP8X4),
+                        lhsT_scale=vs_[b][:, P * cj:P * cj + P],
+                        rhs=wc[:, P * eq:P * eq + P].bitcast(FP8X4),
+                        rhs_scale=ws[:, P * eq:P * eq + P],
+                        start=True, stop=True)
+                nc.scalar.copy(out=vpg[b][:, c, P * eq:P * eq + P, :],
+                               in_=pvp[:].rearrange("p j e -> p e j"))
+
+        def vp_quant(b):
+            nc.vector.quantize_mx(out=vpc[b][:].rearrange("p c e -> p (c e)").bitcast(FP8X4),
+                                  scales=vps[b][:].rearrange("p c e -> p (c e)"),
+                                  in_=vpg[b][:].rearrange("p c e j -> p (c e j)"))
 
         for i in range(4):
             q_norm(i)
@@ -243,16 +252,18 @@ def tile_sinkhornattention_pa_kernel(tc, q_proj, k_proj, v, w_v, out):
         for i in range(4, 8):
             q_norm(i)
             q_tr(i)
+        v_load(0)
         mm(0, 2, 0)
         mm(0, 3, 0)
         spread_half(q2, q2b, 1)
         for cj in range(4, 8):
             k_tr(0, cj)
+            k_norm(0, cj)
         for cj in range(4):
             mm(0, cj, 1)
             clamp(0, cj)
             sqrt_(0, cj)
-            k_norm(0, 4 + cj)
+            k_norm(1, cj)
         for cj in range(4, 8):
             mm(0, cj, 0)
             mm(0, cj, 1)
@@ -260,93 +271,39 @@ def tile_sinkhornattention_pa_kernel(tc, q_proj, k_proj, v, w_v, out):
             sqrt_(0, cj)
             k_tr(1, 2 * (cj - 4))
             k_tr(1, 2 * (cj - 4) + 1)
-            k_norm(1, 2 * (cj - 4))
-            k_norm(1, 2 * (cj - 4) + 1)
+            k_norm(1, cj)
         min_sqrt(0)
-        POOL0 = (0, 2, 4, 6)
         for cj in range(8):
             expo(0, cj)
             mm(1, cj, 0)
             mm(1, cj, 1)
             clamp(1, cj)
             if cj > 0:
-                hilo(0, cj - 1, "g" if cj - 1 in POOL0 else "v")
-        hilo(0, 7, "g" if 7 in POOL0 else "v")
-        small_v(0)
+                hilo(0, cj - 1, (cj - 1) % 2 == 1)
+        hilo(0, 7, True)
         for cj in range(8):
             sqrt_(1, cj)
         min_sqrt(1)
-        w_raw = big.tile([P, 4, D], BF16, name="w_raw", tag="b0", align_bytes=64)
+        for cj in range(8):
+            expo(1, cj)
+        w_raw = big.tile([P, 4, D], BF16, name="w_raw", tag="sG", align_bytes=64)
         nc.sync.dma_start(out=w_raw[:].rearrange("p (u e) c -> p u e c", u=2),
                           in_=w_v.rearrange("(u q e) c -> q u e c", u=2, e=2))
-        wg = big.tile([P, D, 4], BF16, name="wg", tag="b1", align_bytes=64)
-        nc.vector.tensor_copy(out=wg[:], in_=w_raw[:].rearrange("p t c -> p c t"))
-        nc.vector.quantize_mx(out=wc[:].bitcast(FP8X4), scales=ws[:],
-                              in_=wg[:].rearrange("p c t -> p (c t)"))
-        g_mm(0)
-
-        vpc = [const.tile([P, 2, D], U32, name="vpc%d" % b, align_bytes=64) for b in range(B)]
-        vps = [const.tile([P, 2, D], U8, name="vps%d" % b, align_bytes=64) for b in range(B)]
-        v_raw = [None, None]
-        vg = [None, None]
-        vc = [None, None]
-        vs_ = [None, None]
-        vpg = [None, None]
-
-        def v_load(b):
-            v_raw[b] = big.tile([P, 8, D], BF16, name="v_raw", tag=("sA", "sC")[b], align_bytes=64)
-            nc.sync.dma_start(out=v_raw[b][:].rearrange("p (c j) d -> p c j d", c=2),
-                              in_=v[b].rearrange("(c p j) d -> p c j d", c=2, j=4))
-
-        def v_tr(b):
-            vw = v_raw[b][:].bitcast(F32)
-            vg[b] = big.tile([P, N, 4], BF16, name="vg", tag=("sC", "sA")[b], align_bytes=64)
-            vgw = vg[b][:].bitcast(F32)
-            for g in range(4):
-                pv = psum.tile([P, 2, 2, P], F32, name="pv", tag="mm", bufs=3)
-                for a in range(2):
-                    for u in range(2):
-                        nc.tensor.transpose(out=pv[:, a, u, :],
-                                            in_=vw[:, 2 * g + a, P * u:P * u + P],
-                                            identity=ident_f[:])
-                nc.scalar.copy(
-                    out=vgw[:, 256 * g:256 * g + 256, :].rearrange("p (a n) u -> p a n u", a=2),
-                    in_=pv[:].rearrange("p a u n -> p a n u"))
-
-        def v_quant(b):
-            vc[b] = big.tile([P, N], U32, name="vc", tag="vc", align_bytes=64)
-            vs_[b] = big.tile([P, N], U8, name="vs_", tag="vs_", align_bytes=64)
-            nc.vector.quantize_mx(out=vc[b][:].bitcast(FP8X4), scales=vs_[b][:],
-                                  in_=vg[b][:].rearrange("p n t -> p (n t)"))
-
-        def vp_mx(b):
-            vpg[b] = big.tile([P, 2, D, 4], BF16, name="vpg", tag=("sA", "sC")[b], align_bytes=64)
-            for c in range(2):
-                for eq in range(4):
-                    pvp = psum.tile([P, 4, P], F32, name="pvp", tag="mm", bufs=3)
-                    for j in range(4):
-                        cj = 4 * c + j
-                        nc.tensor.matmul_mx(
-                            out=pvp[:, j, :],
-                            lhsT=vc[b][:, P * cj:P * cj + P].bitcast(FP8X4),
-                            lhsT_scale=vs_[b][:, P * cj:P * cj + P],
-                            rhs=wc[:, P * eq:P * eq + P].bitcast(FP8X4),
-                            rhs_scale=ws[:, P * eq:P * eq + P],
-                            start=True, stop=True)
-                    nc.scalar.copy(out=vpg[b][:, c, P * eq:P * eq + P, :],
-                                   in_=pvp[:].rearrange("p j e -> p e j"))
-
-        def vp_quant(b):
-            nc.vector.quantize_mx(out=vpc[b][:].rearrange("p c e -> p (c e)").bitcast(FP8X4),
-                                  scales=vps[b][:].rearrange("p c e -> p (c e)"),
-                                  in_=vpg[b][:].rearrange("p c e j -> p (c e j)"))
-
-        v_load(0)
-
-        junk_box[0] = big.tile([P, T], F32, name="junk", tag="sG", align_bytes=64)
-        NV = 8 - XPE
-        RU_AT = 4
-        POOL1 = (0, 3, 6)
+        wg = big.tile([P, D, 4], BF16, name="wg", tag="sE", align_bytes=64)
+        v_load(1)
+        v_tr(0)
+        junk = big.tile([P, T], F32, name="junk", tag="sA", align_bytes=64)
+        g_update(0)
+        w_quant()
+        v_quant(0)
+        for cj in range(8):
+            hilo(1, cj, cj % 3 != 0)
+            if cj == 5:
+                u_of(0)
+            if cj == 7:
+                v_tr(1)
+        g_update(1)
+        v_quant(1)
 
         def w_scale(b):
             for cj in range(8):
@@ -358,33 +315,20 @@ def tile_sinkhornattention_pa_kernel(tc, q_proj, k_proj, v, w_v, out):
                                             scalar1=vcur[b][:, cj:cj + 1], scalar2=0.0,
                                             op0=ALU.mult, op1=ALU.add)
 
-        def f_begin(b):
-            S[b] = small.tile([P, 8], F32, name="S%d" % b, tag="S%d" % b)
+        for it in range(ITERS - 1):
+            for b in range(B):
+                f_update(b, 2 * it + b)
+                g_update(b)
+                if it == 2 and b == 0:
+                    vp_quant(0)
+                if it == ITERS - 2:
+                    w_scale(b)
 
-        def f_end(b):
-            nc.vector.tensor_reduce(out=S[b][:, 0:XPE], in_=Sp[b][:], axis=AX.X, op=ALU.add)
-            small_v(b)
-            g_mm(b)
-
-        expo(1, 0)
-        r_u_head(0)
-        for x in range(XPE):
-            k_flip(0, x, "v")
-        r_u_tail(0)
-        for cj in range(8):
-            if cj > 0:
-                expo(1, cj)
-            hilo(1, cj, "g" if cj in POOL1 else "v")
-        for x in range(XPE):
-            k_flip(1, x, "s")
-        small_v(1)
-        g_mm(1)
-
-        pig = [None, None]
-        pic = [None, None]
         pis = [const.tile([P, 2, T], U8, name="pis%d" % b, align_bytes=64) for b in range(B)]
+        pig = [big.tile([P, 2, T, 4], BF16, name="pig%d" % b, tag="th%d" % b, align_bytes=64) for b in range(B)]
+        pic = [big.tile([P, 2, T], U32, name="pic%d" % b, tag="tl%d" % b, align_bytes=64) for b in range(B)]
 
-        def pi_half(b, h, between):
+        def pi_mul(b, h):
             sl = slice(512 * h, 512 * h + 512)
             for c in range(2):
                 nc.vector.tensor_tensor(
@@ -392,66 +336,42 @@ def tile_sinkhornattention_pa_kernel(tc, q_proj, k_proj, v, w_v, out):
                     in0=F[b][:, 4 * c:4 * c + 4, sl].rearrange("p j t -> p t j"),
                     in1=ub[b][:, sl].unsqueeze(2).to_broadcast([P, 512, 4]),
                     op=ALU.mult)
-                if c == 0 and between is not None:
-                    r_u(between[0], between[1])
+
+        def pi_quant(b, h):
+            sl = slice(512 * h, 512 * h + 512)
             for c in range(2):
                 nc.vector.quantize_mx(out=pic[b][:, c, sl].bitcast(FP8X4), scales=pis[b][:, c, sl],
                                       in_=pig[b][:, c, sl, :].rearrange("p t j -> p (t j)"))
 
         def out_half(b, h):
             ov = out[b].rearrange("(p i) d -> p i d", i=8)
-            ost = big.tile([P, 4, D], F32, name="ost", tag=("sA", "sC")[h], align_bytes=64)
-            for a in range(4):
-                i = 4 * h + a
-                po = psum.tile([P, D], F32, name="po", tag="mm", bufs=3)
-                for c in range(2):
-                    nc.tensor.matmul_mx(
-                        out=po[:],
-                        lhsT=pic[b][:, c, P * i:P * i + P].bitcast(FP8X4),
-                        lhsT_scale=pis[b][:, c, P * i:P * i + P],
-                        rhs=vpc[b][:, c, :].bitcast(FP8X4),
-                        rhs_scale=vps[b][:, c, :],
-                        start=(c == 0), stop=(c == 1))
-                nc.scalar.copy(out=ost[:, a, :], in_=po[:])
-            nc.sync.dma_start(out=ov[:, 4 * h:4 * h + 4, :], in_=ost[:])
+            for a2 in range(2):
+                ost = big.tile([P, 2, D], F32, name="ost", tag=("sB", "sC", "sE", "sF")[2 * h + a2],
+                               align_bytes=64)
+                for a in range(2):
+                    i = 4 * h + 2 * a2 + a
+                    po = psum.tile([P, D], F32, name="po", tag="ring", bufs=4)
+                    for c in range(2):
+                        nc.tensor.matmul_mx(
+                            out=po[:],
+                            lhsT=pic[b][:, c, P * i:P * i + P].bitcast(FP8X4),
+                            lhsT_scale=pis[b][:, c, P * i:P * i + P],
+                            rhs=vpc[b][:, c, :].bitcast(FP8X4),
+                            rhs_scale=vps[b][:, c, :],
+                            start=(c == 0), stop=(c == 1))
+                    nc.scalar.copy(out=ost[:, a, :], in_=po[:])
+                i0 = 4 * h + 2 * a2
+                nc.sync.dma_start(out=ov[:, i0:i0 + 2, :], in_=ost[:])
 
-        extra = {
-            0: lambda: v_tr(0),
-            1: lambda: v_quant(0),
-            2: lambda: (vp_mx(0), v_load(1)),
-            3: lambda: (vp_quant(0), v_tr(1)),
-            4: lambda: (v_quant(1), vp_mx(1)),
-            5: lambda: vp_quant(1),
-        }
-        runs = [
-            ("f", 0, 0, (1, False)),
-            ("f", 1, 0, (0, False)),
-            ("f", 0, 1, (1, False)),
-            ("f", 1, 1, (0, False)),
-            ("f", 0, 2, (1, False)),
-            ("f", 1, 2, (0, False)),
-            ("f", 0, 3, (1, False)),
-            ("f", 1, 3, (0, True)),
-            ("pi", 0, 0, (1, True)),
-            ("pi", 0, 1, None),
-            ("pi", 1, 0, None),
-            ("pi", 1, 1, None),
-        ]
-        for n_run, (kind, b, idx, between) in enumerate(runs):
-            if kind == "f":
-                f_begin(b)
-                for k in range(NV):
-                    f_stt(b, XPE + k)
-                    if k == RU_AT - 1 and between is not None:
-                        r_u(between[0], between[1])
-                f_end(b)
-                if idx == ITERS - 2:
-                    w_scale(b)
-            else:
-                if idx == 0:
-                    pig[b] = big.tile([P, 2, T, 4], BF16, name="pig%d" % b, tag="th%d" % b, align_bytes=64)
-                    pic[b] = big.tile([P, 2, T], U32, name="pic%d" % b, tag="tl%d" % b, align_bytes=64)
-                pi_half(b, idx, between)
-                out_half(b, idx)
-            if n_run in extra:
-                extra[n_run]()
+        pi_mul(0, 0)
+        vp_quant(1)
+        pi_quant(0, 0)
+        out_half(0, 0)
+        pi_mul(0, 1)
+        u_of(1)
+        pi_quant(0, 1)
+        out_half(0, 1)
+        for h in range(2):
+            pi_mul(1, h)
+            pi_quant(1, h)
+            out_half(1, h)

@@ -70,7 +70,7 @@ def tile_sinkhornattention_pa_kernel(tc, q_proj, k_proj, v, w_v, out):
         nc.sync.dma_start(out=k_raw[1][:, 4:8, :], in_=kv[1][:, 1, :, :])
 
         def norm(src, dst):
-            jn = scr.tile([P, D], BF16, name="jn", tag="jn")
+            jn = scr.tile([P, D], BF16, name="jn", tag="jn", bufs=4)
             nc.scalar.activation(out=jn[:], in_=src, func=ACT.Square, accum_out=dst)
 
         def q_norm(i):
@@ -131,22 +131,25 @@ def tile_sinkhornattention_pa_kernel(tc, q_proj, k_proj, v, w_v, out):
                                  bias=mn[b][:, cj:cj + 1], scale=-1.0,
                                  accum_out=sums[b][:, cj:cj + 1])
 
-        def hilo(b, cj, on_vector):
-            if on_vector:
-                nc.vector.tensor_copy(out=TH[b][:, cj, :], in_=F[b][:, cj, :])
-                nc.vector.tensor_tensor(out=TL[b][:, cj, :], in0=F[b][:, cj, :], in1=TH[b][:, cj, :],
-                                        op=ALU.subtract)
-            else:
-                nc.gpsimd.tensor_scalar(out=TH[b][:, cj, :], in0=F[b][:, cj, :], scalar1=1.0,
-                                        scalar2=0.0, op0=ALU.mult, op1=ALU.add)
-                nc.gpsimd.tensor_tensor(out=TL[b][:, cj, :], in0=F[b][:, cj, :], in1=TH[b][:, cj, :],
-                                        op=ALU.subtract)
+        def hi(b, cj):
+            nc.vector.tensor_copy(out=TH[b][:, cj, :], in_=F[b][:, cj, :])
+
+        def lo(b, cj):
+            nc.vector.tensor_tensor(out=TL[b][:, cj, :], in0=F[b][:, cj, :], in1=TH[b][:, cj, :],
+                                    op=ALU.subtract)
+
+        def hilo_gpsimd(b, cj):
+            nc.gpsimd.tensor_scalar(out=TH[b][:, cj, :], in0=F[b][:, cj, :], scalar1=1.0,
+                                    scalar2=0.0, op0=ALU.mult, op1=ALU.add)
+            nc.gpsimd.tensor_tensor(out=TL[b][:, cj, :], in0=F[b][:, cj, :], in1=TH[b][:, cj, :],
+                                    op=ALU.subtract)
 
         def g_update(b):
             vcur[b] = small.tile([P, 8], F32, name="v%d" % b, tag="v%d" % b)
             nc.vector.reciprocal(out=vcur[b][:], in_=sums[b][:])
             vsp[b] = small.tile([P, 8, 2], BF16, name="vsp%d" % b, tag="vsp%d" % b)
-            nc.vector.tensor_copy(out=vsp[b][:, :, 0], in_=vcur[b][:])
+            with nc.allow_low_precision(reason="the bf16 head of v; its tail goes into the second column"):
+                nc.vector.reciprocal(out=vsp[b][:, :, 0], in_=sums[b][:])
             nc.vector.tensor_tensor(out=vsp[b][:, :, 1], in0=vcur[b][:], in1=vsp[b][:, :, 0],
                                     op=ALU.subtract)
             Rt[b] = psum.tile([P, 8, 2], F32, name="R", tag="mv%d" % b, bufs=1)
@@ -157,20 +160,27 @@ def tile_sinkhornattention_pa_kernel(tc, q_proj, k_proj, v, w_v, out):
                                          rhs=vsp[b][:, cj, :],
                                          start=(cj == 0 and s == 0), stop=(cj == 7 and s == 1))
 
+        rcur = [None, None]
+
+        def r_of(b):
+            rcur[b] = small.tile([P, 8], F32, name="r%d" % b, tag="r%d" % b)
+            nc.vector.tensor_reduce(out=rcur[b][:], in_=Rt[b][:], axis=AX.X, op=ALU.add)
+
         def u_of(b):
-            r = small.tile([P, 8], F32, name="r%d" % b, tag="r%d" % b)
-            nc.vector.tensor_reduce(out=r[:], in_=Rt[b][:], axis=AX.X, op=ALU.add)
             u = small.tile([P, 8], F32, name="u%d" % b, tag="u%d" % b)
-            nc.vector.reciprocal(out=u[:], in_=r[:])
+            nc.vector.reciprocal(out=u[:], in_=rcur[b][:])
             for hh in range(2):
                 spread_half(u, ub[b], hh)
 
         def f_update(b, step):
             sums[b] = small.tile([P, 8], F32, name="sums%d" % b, tag="sums%d" % b)
             for cj in range(8):
+                if cj == RU_AT - 1:
+                    r_of(1 - b)
                 if cj == RU_AT:
                     u_of(1 - b)
                     vp_eighth(step)
+                junk = scr.tile([P, T], F32, name="junk", tag="junk", bufs=3)
                 nc.vector.scalar_tensor_tensor(
                     out=junk[:], in0=F[b][:, cj, :], scalar=1.0, in1=ub[b][:],
                     op0=ALU.mult, op1=ALU.mult, accum_out=sums[b][:, cj:cj + 1])
@@ -261,26 +271,35 @@ def tile_sinkhornattention_pa_kernel(tc, q_proj, k_proj, v, w_v, out):
             k_norm(0, cj)
         for cj in range(4):
             mm(0, cj, 1)
-            clamp(0, cj)
-            sqrt_(0, cj)
+            if cj > 0:
+                clamp(0, cj - 1)
+                sqrt_(0, cj - 1)
             k_norm(1, cj)
         for cj in range(4, 8):
             mm(0, cj, 0)
+            clamp(0, cj - 1)
+            sqrt_(0, cj - 1)
             mm(0, cj, 1)
-            clamp(0, cj)
-            sqrt_(0, cj)
             k_tr(1, 2 * (cj - 4))
             k_tr(1, 2 * (cj - 4) + 1)
             k_norm(1, cj)
+        clamp(0, 7)
+        sqrt_(0, 7)
         min_sqrt(0)
         for cj in range(8):
             expo(0, cj)
             mm(1, cj, 0)
-            mm(1, cj, 1)
-            clamp(1, cj)
             if cj > 0:
-                hilo(0, cj - 1, (cj - 1) % 2 == 1)
-        hilo(0, 7, True)
+                clamp(1, cj - 1)
+            if cj % 2 == 0 and cj > 0:
+                hi(0, cj - 1)
+            mm(1, cj, 1)
+            if cj % 2 == 0 and cj > 0:
+                lo(0, cj - 1)
+            if cj % 2 == 1:
+                hilo_gpsimd(0, cj - 1)
+        clamp(1, 7)
+        hi(0, 7)
         for cj in range(8):
             sqrt_(1, cj)
         min_sqrt(1)
@@ -292,16 +311,25 @@ def tile_sinkhornattention_pa_kernel(tc, q_proj, k_proj, v, w_v, out):
         wg = big.tile([P, D, 4], BF16, name="wg", tag="sE", align_bytes=64)
         v_load(1)
         v_tr(0)
-        junk = big.tile([P, T], F32, name="junk", tag="sA", align_bytes=64)
+        lo(0, 7)
         g_update(0)
         w_quant()
         v_quant(0)
         for cj in range(8):
-            hilo(1, cj, cj % 3 != 0)
+            if cj % 3 == 0:
+                hilo_gpsimd(1, cj)
+            else:
+                hi(1, cj)
+            if cj == 5:
+                r_of(0)
+            if cj % 3 == 2:
+                lo(1, cj - 1)
+            if cj % 3 == 1 and cj > 1:
+                lo(1, cj - 2)
             if cj == 5:
                 u_of(0)
-            if cj == 7:
-                v_tr(1)
+        lo(1, 7)
+        v_tr(1)
         g_update(1)
         v_quant(1)
 
@@ -367,6 +395,7 @@ def tile_sinkhornattention_pa_kernel(tc, q_proj, k_proj, v, w_v, out):
         vp_quant(1)
         pi_quant(0, 0)
         out_half(0, 0)
+        r_of(1)
         pi_mul(0, 1)
         u_of(1)
         pi_quant(0, 1)

@@ -21,7 +21,11 @@ ITERS = 5
 TINY = 2.0 ** -100
 FLOPS = 2 * B * T * N * D + 2 * B * N * D * D + 2 * B * T * N * D
 
-RU_AT = 7
+NV = 6
+
+
+def col(cj):
+    return cj if cj < NV else 8 + cj - NV
 
 
 def tile_sinkhornattention_pa_kernel(tc, q_proj, k_proj, v, w_v, out):
@@ -54,8 +58,13 @@ def tile_sinkhornattention_pa_kernel(tc, q_proj, k_proj, v, w_v, out):
         TL = [big.tile([P, 8, T], BF16, name="TL%d" % b, tag="tl%d" % b, align_bytes=64) for b in range(B)]
         minsq = [const.tile([P, 8], F32, name="minsq%d" % b) for b in range(B)]
         mn = [const.tile([P, 8], F32, name="mn%d" % b) for b in range(B)]
-        ub = [big.tile([P, T], F32, name="ub%d" % b, tag="ub%d" % b) for b in range(B)]
-        sums = [None, None]
+        ub = [[None, None], [None, None]]
+        halves = [None, None]
+        sums = [const.tile([P, 16], F32, name="sums%d" % b) for b in range(B)]
+        first = [const.tile([P, 16], F32, name="first%d" % b) for b in range(B)]
+        for b in range(B):
+            nc.vector.memset(sums[b][:], 1.0)
+            nc.vector.memset(first[b][:], 1.0)
         vcur = [None, None]
         vsp = [None, None]
         Rt = [None, None]
@@ -94,17 +103,21 @@ def tile_sinkhornattention_pa_kernel(tc, q_proj, k_proj, v, w_v, out):
                                     identity=ident_bf[:])
             nc.vector.tensor_copy(out=kT[b][:, :, P * cj:P * cj + P], in_=pt[:])
 
-        def spread_half(vec, dst, hh):
-            pb = psum.tile([P, 512], F32, name="pb", tag="tr", bufs=2)
+        def spread_half(vec, hh, tag):
+            pb = psum.tile([P, 512], F32, name="pb", tag=tag, bufs=2)
             for a in range(4):
                 i = 4 * hh + a
                 nc.tensor.transpose(out=pb[:, P * a:P * a + P],
                                     in_=vec[:, i:i + 1].to_broadcast([P, P]),
                                     identity=ident_f[:])
-            nc.scalar.copy(out=dst[:, 512 * hh:512 * hh + 512], in_=pb[:])
+            return pb
+
+        def q2_spread(hh):
+            pb = spread_half(q2, hh, "tr")
+            nc.scalar.copy(out=q2b[:, 512 * hh:512 * hh + 512], in_=pb[:])
 
         def mm(b, cj, h):
-            pq = psum.tile([P, 512], F32, name="pq", tag="ring", bufs=4)
+            pq = psum.tile([P, 512], F32, name="pq", tag="ub%d" % h, bufs=2)
             for dk in range(4):
                 nc.tensor.matmul(out=pq[:], lhsT=kT[b][:, dk, P * cj:P * cj + P],
                                  rhs=qT[:, dk, 512 * h:512 * h + 512],
@@ -124,12 +137,11 @@ def tile_sinkhornattention_pa_kernel(tc, q_proj, k_proj, v, w_v, out):
 
         def min_sqrt(b):
             nc.scalar.activation(out=mn[b][:], in_=minsq[b][:], func=ACT.Sqrt)
-            sums[b] = small.tile([P, 8], F32, name="sums%d" % b, tag="sums%d" % b)
 
         def expo(b, cj):
             nc.scalar.activation(out=F[b][:, cj, :], in_=F[b][:, cj, :], func=ACT.Exp,
                                  bias=mn[b][:, cj:cj + 1], scale=-1.0,
-                                 accum_out=sums[b][:, cj:cj + 1])
+                                 accum_out=first[b][:, col(cj):col(cj) + 1])
 
         def hi(b, cj):
             nc.vector.tensor_copy(out=TH[b][:, cj, :], in_=F[b][:, cj, :])
@@ -138,18 +150,22 @@ def tile_sinkhornattention_pa_kernel(tc, q_proj, k_proj, v, w_v, out):
             nc.vector.tensor_tensor(out=TL[b][:, cj, :], in0=F[b][:, cj, :], in1=TH[b][:, cj, :],
                                     op=ALU.subtract)
 
+        def lo_gpsimd(b, cj):
+            nc.gpsimd.tensor_tensor(out=TL[b][:, cj, :], in0=F[b][:, cj, :], in1=TH[b][:, cj, :],
+                                    op=ALU.subtract)
+
         def hilo_gpsimd(b, cj):
             nc.gpsimd.tensor_scalar(out=TH[b][:, cj, :], in0=F[b][:, cj, :], scalar1=1.0,
                                     scalar2=0.0, op0=ALU.mult, op1=ALU.add)
             nc.gpsimd.tensor_tensor(out=TL[b][:, cj, :], in0=F[b][:, cj, :], in1=TH[b][:, cj, :],
                                     op=ALU.subtract)
 
-        def g_update(b):
-            vcur[b] = small.tile([P, 8], F32, name="v%d" % b, tag="v%d" % b)
-            nc.vector.reciprocal(out=vcur[b][:], in_=sums[b][:])
-            vsp[b] = small.tile([P, 8, 2], BF16, name="vsp%d" % b, tag="vsp%d" % b)
+        def g_update(b, src):
+            vcur[b] = small.tile([P, 16], F32, name="v%d" % b, tag="v%d" % b)
+            nc.vector.reciprocal(out=vcur[b][:], in_=src[:])
+            vsp[b] = small.tile([P, 16, 2], BF16, name="vsp%d" % b, tag="vsp%d" % b)
             with nc.allow_low_precision(reason="the bf16 head of v; its tail goes into the second column"):
-                nc.vector.reciprocal(out=vsp[b][:, :, 0], in_=sums[b][:])
+                nc.vector.reciprocal(out=vsp[b][:, :, 0], in_=src[:])
             nc.vector.tensor_tensor(out=vsp[b][:, :, 1], in0=vcur[b][:], in1=vsp[b][:, :, 0],
                                     op=ALU.subtract)
             Rt[b] = psum.tile([P, 8, 2], F32, name="R", tag="mv%d" % b, bufs=1)
@@ -157,7 +173,7 @@ def tile_sinkhornattention_pa_kernel(tc, q_proj, k_proj, v, w_v, out):
                 for cj in range(8):
                     for s, piece in enumerate((TH[b], TL[b])):
                         nc.tensor.matmul(out=Rt[b][:, i, :], lhsT=piece[:, cj, P * i:P * i + P],
-                                         rhs=vsp[b][:, cj, :],
+                                         rhs=vsp[b][:, col(cj), :],
                                          start=(cj == 0 and s == 0), stop=(cj == 7 and s == 1))
 
         rcur = [None, None]
@@ -170,20 +186,34 @@ def tile_sinkhornattention_pa_kernel(tc, q_proj, k_proj, v, w_v, out):
             u = small.tile([P, 8], F32, name="u%d" % b, tag="u%d" % b)
             nc.vector.reciprocal(out=u[:], in_=rcur[b][:])
             for hh in range(2):
-                spread_half(u, ub[b], hh)
+                ub[b][hh] = spread_half(u, hh, "ub%d" % b)
+
+        def f_side(b):
+            for hh in range(2):
+                nc.scalar.copy(out=ubs[:, b, 512 * hh:512 * hh + 512], in_=ub[b][hh][:])
+            for cj in range(NV, 8):
+                prod = scr.tile([P, T], F32, name="prod", tag="prod", bufs=2)
+                nc.gpsimd.tensor_tensor(out=prod[:], in0=F[b][:, cj, :], in1=ubs[:, b, :], op=ALU.mult)
+                nc.scalar.activation(out=prod[:], in_=prod[:], func=ACT.Copy,
+                                     accum_out=sums[b][:, col(cj):col(cj) + 1])
 
         def f_update(b, step):
-            sums[b] = small.tile([P, 8], F32, name="sums%d" % b, tag="sums%d" % b)
-            for cj in range(8):
-                if cj == RU_AT - 1:
-                    r_of(1 - b)
-                if cj == RU_AT:
-                    u_of(1 - b)
-                    vp_eighth(step)
-                junk = scr.tile([P, T], F32, name="junk", tag="junk", bufs=3)
-                nc.vector.scalar_tensor_tensor(
-                    out=junk[:], in0=F[b][:, cj, :], scalar=1.0, in1=ub[b][:],
-                    op0=ALU.mult, op1=ALU.mult, accum_out=sums[b][:, cj:cj + 1])
+            halves[b] = small.tile([P, NV, 2], F32, name="halves%d" % b, tag="halves%d" % b)
+            for cj in range(NV):
+                for hh in range(2):
+                    if 2 * cj + hh == 2 * NV - 2:
+                        r_of(1 - b)
+                    if 2 * cj + hh == 2 * NV - 2 + 1:
+                        u_of(1 - b)
+                        if step < 7:
+                            f_side(1 - b)
+                        vp_eighth(step)
+                    junk = scr.tile([P, 512], F32, name="junk", tag="junk", bufs=4)
+                    nc.vector.scalar_tensor_tensor(
+                        out=junk[:], in0=F[b][:, cj, 512 * hh:512 * hh + 512], scalar=1.0,
+                        in1=ub[b][hh][:], op0=ALU.mult, op1=ALU.mult,
+                        accum_out=halves[b][:, cj, hh:hh + 1])
+            nc.vector.tensor_reduce(out=sums[b][:, 0:NV], in_=halves[b][:], axis=AX.X, op=ALU.add)
 
         wc = const.tile([P, D], U32, name="wc", align_bytes=64)
         ws = const.tile([P, D], U8, name="ws", align_bytes=64)
@@ -209,7 +239,7 @@ def tile_sinkhornattention_pa_kernel(tc, q_proj, k_proj, v, w_v, out):
             vg[b] = big.tile([P, N, 4], BF16, name="vg", tag=("sB", "sC")[b], align_bytes=64)
             vgw = vg[b][:].bitcast(F32)
             for g in range(4):
-                pv = psum.tile([P, 2, 2, P], F32, name="pv", tag="ring", bufs=4)
+                pv = psum.tile([P, 2, 2, P], F32, name="pv", tag="tr", bufs=2)
                 for a in range(2):
                     for u in range(2):
                         nc.tensor.transpose(out=pv[:, a, u, :],
@@ -231,7 +261,7 @@ def tile_sinkhornattention_pa_kernel(tc, q_proj, k_proj, v, w_v, out):
             if step % 4 == 0:
                 vpg[b] = big.tile([P, 2, D, 4], BF16, name="vpg", tag=("sE", "sF")[b], align_bytes=64)
             for eq in (2 * (step % 2), 2 * (step % 2) + 1):
-                pvp = psum.tile([P, 4, P], F32, name="pvp", tag="ring", bufs=4)
+                pvp = psum.tile([P, 4, P], F32, name="pvp", tag="tr", bufs=2)
                 for j in range(4):
                     cj = 4 * c + j
                     nc.tensor.matmul_mx(
@@ -254,7 +284,7 @@ def tile_sinkhornattention_pa_kernel(tc, q_proj, k_proj, v, w_v, out):
             q_tr(i)
         for cj in range(4):
             k_tr(0, cj)
-        spread_half(q2, q2b, 0)
+        q2_spread(0)
         for cj in range(4):
             k_norm(0, cj)
         mm(0, 0, 0)
@@ -265,7 +295,7 @@ def tile_sinkhornattention_pa_kernel(tc, q_proj, k_proj, v, w_v, out):
         v_load(0)
         mm(0, 2, 0)
         mm(0, 3, 0)
-        spread_half(q2, q2b, 1)
+        q2_spread(1)
         for cj in range(4, 8):
             k_tr(0, cj)
             k_norm(0, cj)
@@ -291,15 +321,13 @@ def tile_sinkhornattention_pa_kernel(tc, q_proj, k_proj, v, w_v, out):
             mm(1, cj, 0)
             if cj > 0:
                 clamp(1, cj - 1)
-            if cj % 2 == 0 and cj > 0:
+            if cj > 0:
                 hi(0, cj - 1)
+                lo_gpsimd(0, cj - 1)
             mm(1, cj, 1)
-            if cj % 2 == 0 and cj > 0:
-                lo(0, cj - 1)
-            if cj % 2 == 1:
-                hilo_gpsimd(0, cj - 1)
         clamp(1, 7)
         hi(0, 7)
+        lo_gpsimd(0, 7)
         for cj in range(8):
             sqrt_(1, cj)
         min_sqrt(1)
@@ -311,42 +339,40 @@ def tile_sinkhornattention_pa_kernel(tc, q_proj, k_proj, v, w_v, out):
         wg = big.tile([P, D, 4], BF16, name="wg", tag="sE", align_bytes=64)
         v_load(1)
         v_tr(0)
-        lo(0, 7)
-        g_update(0)
+        ubs = big.tile([P, B, T], F32, name="ubs", tag="sA", align_bytes=64)
+        g_update(0, first[0])
         w_quant()
         v_quant(0)
         for cj in range(8):
-            if cj % 3 == 0:
-                hilo_gpsimd(1, cj)
-            else:
-                hi(1, cj)
+            hi(1, cj)
             if cj == 5:
                 r_of(0)
-            if cj % 3 == 2:
+            if cj < 5:
+                lo_gpsimd(1, cj)
+            if cj > 5:
                 lo(1, cj - 1)
-            if cj % 3 == 1 and cj > 1:
-                lo(1, cj - 2)
             if cj == 5:
                 u_of(0)
+                f_side(0)
         lo(1, 7)
         v_tr(1)
-        g_update(1)
+        g_update(1, first[1])
         v_quant(1)
 
         def w_scale(b):
             for cj in range(8):
                 if cj % 2 == 0:
                     nc.scalar.activation(out=F[b][:, cj, :], in_=F[b][:, cj, :], func=ACT.Copy,
-                                         scale=vcur[b][:, cj:cj + 1])
+                                         scale=vcur[b][:, col(cj):col(cj) + 1])
                 else:
                     nc.gpsimd.tensor_scalar(out=F[b][:, cj, :], in0=F[b][:, cj, :],
-                                            scalar1=vcur[b][:, cj:cj + 1], scalar2=0.0,
+                                            scalar1=vcur[b][:, col(cj):col(cj) + 1], scalar2=0.0,
                                             op0=ALU.mult, op1=ALU.add)
 
         for it in range(ITERS - 1):
             for b in range(B):
                 f_update(b, 2 * it + b)
-                g_update(b)
+                g_update(b, sums[b])
                 if it == 2 and b == 0:
                     vp_quant(0)
                 if it == ITERS - 2:
@@ -362,7 +388,7 @@ def tile_sinkhornattention_pa_kernel(tc, q_proj, k_proj, v, w_v, out):
                 nc.vector.tensor_tensor(
                     out=pig[b][:, c, sl, :],
                     in0=F[b][:, 4 * c:4 * c + 4, sl].rearrange("p j t -> p t j"),
-                    in1=ub[b][:, sl].unsqueeze(2).to_broadcast([P, 512, 4]),
+                    in1=ub[b][h][:].unsqueeze(2).to_broadcast([P, 512, 4]),
                     op=ALU.mult)
 
         def pi_quant(b, h):
@@ -378,7 +404,7 @@ def tile_sinkhornattention_pa_kernel(tc, q_proj, k_proj, v, w_v, out):
                                align_bytes=64)
                 for a in range(2):
                     i = 4 * h + 2 * a2 + a
-                    po = psum.tile([P, D], F32, name="po", tag="ring", bufs=4)
+                    po = psum.tile([P, D], F32, name="po", tag="tr", bufs=2)
                     for c in range(2):
                         nc.tensor.matmul_mx(
                             out=po[:],

@@ -43,6 +43,9 @@ def tile_sinkhornattention_pa_kernel(tc, q_proj, k_proj, v, w_v, out):
         ident_f = const.tile([P, P], F32, name="ident_f")
         make_identity(nc, ident_f[:])
 
+        zeros = const.tile([P, 16], BF16, name="zeros")
+        nc.vector.memset(zeros[:], 0.0)
+
         q_raw = big.tile([P, 8, D], BF16, name="q_raw", tag="sA", align_bytes=64)
         k_raw = [big.tile([P, 8, D], BF16, name="k_raw%d" % b, tag=("sB", "sC")[b], align_bytes=64)
                  for b in range(B)]
@@ -169,12 +172,14 @@ def tile_sinkhornattention_pa_kernel(tc, q_proj, k_proj, v, w_v, out):
             nc.vector.tensor_tensor(out=vsp[b][:, :, 1], in0=vcur[b][:], in1=vsp[b][:, :, 0],
                                     op=ALU.subtract)
             Rt[b] = psum.tile([P, 8, 2], F32, name="R", tag="mv%d" % b, bufs=1)
-            for i in range(8):
-                for cj in range(8):
-                    for s, piece in enumerate((TH[b], TL[b])):
+            nc.tensor.matmul(out=Rt[b][:].rearrange("p i s -> p (i s)"), lhsT=ident_bf[:], rhs=zeros[:],
+                             start=True, stop=False)
+            for cj in range(8):
+                for s, piece in enumerate((TH[b], TL[b])):
+                    for i in range(8):
                         nc.tensor.matmul(out=Rt[b][:, i, :], lhsT=piece[:, cj, P * i:P * i + P],
                                          rhs=vsp[b][:, col(cj), :],
-                                         start=(cj == 0 and s == 0), stop=(cj == 7 and s == 1))
+                                         start=False, stop=(cj == 7 and s == 1 and i == 7))
 
         rcur = [None, None]
 

@@ -391,9 +391,9 @@ def tile_sinkhornattention_pa_kernel(tc, q_proj, k_proj, v, w_v, out):
             sl = slice(512 * h, 512 * h + 512)
             for c in range(2):
                 nc.vector.tensor_tensor(
-                    out=pig[b][:, c, sl, :],
-                    in0=F[b][:, 4 * c:4 * c + 4, sl].rearrange("p j t -> p t j"),
-                    in1=ub[b][h][:].unsqueeze(2).to_broadcast([P, 512, 4]),
+                    out=pig[b][:, c, sl, :].rearrange("p (g i) j -> p g j i", i=4),
+                    in0=F[b][:, 4 * c:4 * c + 4, sl].rearrange("p j (g i) -> p g j i", i=4),
+                    in1=ub[b][h][:].rearrange("p (g i) -> p g i", i=4).unsqueeze(2).to_broadcast([P, 128, 4, 4]),
                     op=ALU.mult)
 
         def pi_quant(b, h):

@@ -18,14 +18,15 @@ T = 1024
 N = 1024
 D = 512
 ITERS = 5
-TINY = 2.0 ** -100
+TINY = 2.0 ** -90
+HAIR = 2.0 ** -22
 FLOPS = 2 * B * T * N * D + 2 * B * N * D * D + 2 * B * T * N * D
 
+QA = (2, 1)
+SPLIT_GPSIMD = 5
 NV = 6
-
-
-def col(cj):
-    return cj if cj < NV else 8 + cj - NV
+EARLY = 4
+STEPS = 2 * (ITERS - 1)
 
 
 def tile_sinkhornattention_pa_kernel(tc, q_proj, k_proj, v, w_v, out):
@@ -42,7 +43,6 @@ def tile_sinkhornattention_pa_kernel(tc, q_proj, k_proj, v, w_v, out):
         make_identity(nc, ident_bf[:])
         ident_f = const.tile([P, P], F32, name="ident_f")
         make_identity(nc, ident_f[:])
-
         zeros = const.tile([P, 16], BF16, name="zeros")
         nc.vector.memset(zeros[:], 0.0)
 
@@ -55,22 +55,24 @@ def tile_sinkhornattention_pa_kernel(tc, q_proj, k_proj, v, w_v, out):
               for b in range(B)]
         q2 = const.tile([P, 8], F32, name="q2")
         k2 = [const.tile([P, 8], F32, name="k2_%d" % b) for b in range(B)]
+        floor = [const.tile([P, 8], F32, name="floor%d" % b) for b in range(B)]
+        minh = [const.tile([P, 8, 2], F32, name="minh%d" % b) for b in range(B)]
         q2b = big.tile([P, T], F32, name="q2b", tag="sG", align_bytes=64)
         F = [big.tile([P, 8, T], F32, name="F%d" % b, tag="F%d" % b) for b in range(B)]
         TH = [big.tile([P, 8, T], BF16, name="TH%d" % b, tag="th%d" % b, align_bytes=64) for b in range(B)]
         TL = [big.tile([P, 8, T], BF16, name="TL%d" % b, tag="tl%d" % b, align_bytes=64) for b in range(B)]
         minsq = [const.tile([P, 8], F32, name="minsq%d" % b) for b in range(B)]
         mn = [const.tile([P, 8], F32, name="mn%d" % b) for b in range(B)]
-        ub = [[None, None], [None, None]]
+        sums = [const.tile([P, 8], F32, name="sums%d" % b) for b in range(B)]
+        first = [const.tile([P, 8], F32, name="first%d" % b) for b in range(B)]
+        bank = [None, None]
         halves = [None, None]
-        sums = [const.tile([P, 16], F32, name="sums%d" % b) for b in range(B)]
-        first = [const.tile([P, 16], F32, name="first%d" % b) for b in range(B)]
-        for b in range(B):
-            nc.vector.memset(sums[b][:], 1.0)
-            nc.vector.memset(first[b][:], 1.0)
+        rcur = [None, None]
+        ucur = [None, None]
+        ub = [[None, None], [None, None]]
+        ubs = [None]
         vcur = [None, None]
         vsp = [None, None]
-        Rt = [None, None]
 
         qv = q_proj.rearrange("(p i) d -> p i d", i=8)
         kv = [k_proj[b].rearrange("(c p j) d -> p c j d", c=2, j=4) for b in range(B)]
@@ -82,7 +84,7 @@ def tile_sinkhornattention_pa_kernel(tc, q_proj, k_proj, v, w_v, out):
         nc.sync.dma_start(out=k_raw[1][:, 4:8, :], in_=kv[1][:, 1, :, :])
 
         def norm(src, dst):
-            jn = scr.tile([P, D], BF16, name="jn", tag="jn", bufs=4)
+            jn = scr.tile([P, D], BF16, name="jn", tag="jn", bufs=2)
             nc.scalar.activation(out=jn[:], in_=src, func=ACT.Square, accum_out=dst)
 
         def q_norm(i):
@@ -106,8 +108,8 @@ def tile_sinkhornattention_pa_kernel(tc, q_proj, k_proj, v, w_v, out):
                                     identity=ident_bf[:])
             nc.vector.tensor_copy(out=kT[b][:, :, P * cj:P * cj + P], in_=pt[:])
 
-        def spread_half(vec, hh, tag):
-            pb = psum.tile([P, 512], F32, name="pb", tag=tag, bufs=2)
+        def spread_half(vec, hh, tag, bufs):
+            pb = psum.tile([P, 512], F32, name="pb", tag=tag, bufs=bufs)
             for a in range(4):
                 i = 4 * hh + a
                 nc.tensor.transpose(out=pb[:, P * a:P * a + P],
@@ -116,35 +118,61 @@ def tile_sinkhornattention_pa_kernel(tc, q_proj, k_proj, v, w_v, out):
             return pb
 
         def q2_spread(hh):
-            pb = spread_half(q2, hh, "tr")
-            nc.scalar.copy(out=q2b[:, 512 * hh:512 * hh + 512], in_=pb[:])
+            pb = spread_half(q2, hh, "tr", 2)
+            nc.vector.tensor_copy(out=q2b[:, 512 * hh:512 * hh + 512], in_=pb[:])
+
+        def added_in_psum(b, cj):
+            return cj >= 8 - QA[b]
 
         def mm(b, cj, h):
-            pq = psum.tile([P, 512], F32, name="pq", tag="ub%d" % h, bufs=2)
+            pq = psum.tile([P, 512], F32, name="pq", tag="qk", bufs=4)
             for dk in range(4):
                 nc.tensor.matmul(out=pq[:], lhsT=kT[b][:, dk, P * cj:P * cj + P],
                                  rhs=qT[:, dk, 512 * h:512 * h + 512],
-                                 start=(dk == 0), stop=(dk == 3))
-            nc.vector.scalar_tensor_tensor(
-                out=F[b][:, cj, 512 * h:512 * h + 512], in0=pq[:],
-                scalar=k2[b][:, cj:cj + 1], in1=q2b[:, 512 * h:512 * h + 512],
-                op0=ALU.add, op1=ALU.add)
+                                 start=(dk == 0), stop=(dk == 3 and not added_in_psum(b, cj)))
+            if added_in_psum(b, cj):
+                for a in range(4):
+                    i = 4 * h + a
+                    nc.tensor.matmul(out=pq[:, P * a:P * a + P], lhsT=q2[:, i:i + 1].to_broadcast([P, P]),
+                                     rhs=ident_f[:], is_transpose=True, start=False, stop=(a == 3))
+                nc.vector.tensor_scalar(
+                    out=F[b][:, cj, 512 * h:512 * h + 512], in0=pq[:],
+                    scalar1=floor[b][:, cj:cj + 1], scalar2=None, op0=ALU.max, op1=ALU.min,
+                    accum_out=minh[b][:, cj, h:h + 1])
+            else:
+                nc.vector.scalar_tensor_tensor(
+                    out=F[b][:, cj, 512 * h:512 * h + 512], in0=pq[:],
+                    scalar=k2[b][:, cj:cj + 1], in1=q2b[:, 512 * h:512 * h + 512],
+                    op0=ALU.add, op1=ALU.add)
+
+        def floors(b):
+            nc.vector.tensor_scalar(out=k2[b][:, 4:8], in0=k2[b][:, 4:8], scalar1=TINY, scalar2=None, op0=ALU.max)
+            nc.vector.tensor_scalar(out=floor[b][:, 4:8], in0=k2[b][:, 4:8], scalar1=HAIR - 1.0, scalar2=None,
+                                    op0=ALU.mult)
 
         def clamp(b, cj):
-            nc.vector.tensor_scalar(out=F[b][:, cj, :], in0=F[b][:, cj, :], scalar1=TINY,
-                                    scalar2=None, op0=ALU.max, op1=ALU.min,
-                                    accum_out=minsq[b][:, cj:cj + 1])
+            if not added_in_psum(b, cj):
+                nc.vector.tensor_scalar(out=F[b][:, cj, :], in0=F[b][:, cj, :], scalar1=TINY,
+                                        scalar2=None, op0=ALU.max, op1=ALU.min,
+                                        accum_out=minsq[b][:, cj:cj + 1])
 
         def sqrt_(b, cj):
-            nc.scalar.activation(out=F[b][:, cj, :], in_=F[b][:, cj, :], func=ACT.Sqrt)
+            if added_in_psum(b, cj):
+                nc.scalar.activation(out=F[b][:, cj, :], in_=F[b][:, cj, :], func=ACT.Sqrt,
+                                     bias=k2[b][:, cj:cj + 1])
+            else:
+                nc.scalar.activation(out=F[b][:, cj, :], in_=F[b][:, cj, :], func=ACT.Sqrt)
 
         def min_sqrt(b):
+            sl = slice(8 - QA[b], 8)
+            nc.vector.tensor_reduce(out=minsq[b][:, sl], in_=minh[b][:, sl, :], axis=AX.X, op=ALU.min)
+            nc.vector.tensor_tensor(out=minsq[b][:, sl], in0=minsq[b][:, sl], in1=k2[b][:, sl], op=ALU.add)
             nc.scalar.activation(out=mn[b][:], in_=minsq[b][:], func=ACT.Sqrt)
 
         def expo(b, cj):
             nc.scalar.activation(out=F[b][:, cj, :], in_=F[b][:, cj, :], func=ACT.Exp,
                                  bias=mn[b][:, cj:cj + 1], scale=-1.0,
-                                 accum_out=first[b][:, col(cj):col(cj) + 1])
+                                 accum_out=first[b][:, cj:cj + 1])
 
         def hi(b, cj):
             nc.vector.tensor_copy(out=TH[b][:, cj, :], in_=F[b][:, cj, :])
@@ -153,72 +181,77 @@ def tile_sinkhornattention_pa_kernel(tc, q_proj, k_proj, v, w_v, out):
             nc.vector.tensor_tensor(out=TL[b][:, cj, :], in0=F[b][:, cj, :], in1=TH[b][:, cj, :],
                                     op=ALU.subtract)
 
-        def lo_gpsimd(b, cj):
-            nc.gpsimd.tensor_tensor(out=TL[b][:, cj, :], in0=F[b][:, cj, :], in1=TH[b][:, cj, :],
-                                    op=ALU.subtract)
-
         def hilo_gpsimd(b, cj):
             nc.gpsimd.tensor_scalar(out=TH[b][:, cj, :], in0=F[b][:, cj, :], scalar1=1.0,
                                     scalar2=0.0, op0=ALU.mult, op1=ALU.add)
             nc.gpsimd.tensor_tensor(out=TL[b][:, cj, :], in0=F[b][:, cj, :], in1=TH[b][:, cj, :],
                                     op=ALU.subtract)
 
-        def g_update(b, src):
-            vcur[b] = small.tile([P, 16], F32, name="v%d" % b, tag="v%d" % b)
-            nc.vector.reciprocal(out=vcur[b][:], in_=src[:])
-            vsp[b] = small.tile([P, 16, 2], BF16, name="vsp%d" % b, tag="vsp%d" % b)
+        def v_first(b):
+            vcur[b] = small.tile([P, 8], F32, name="v%d" % b, tag="v%d" % b)
+            vsp[b] = small.tile([P, 8, 2], BF16, name="vsp%d" % b, tag="vsp%d" % b)
+            v_rec(b, first[b], 0, 8)
+            v_lo(b, 0, 8)
+
+        def v_rec(b, src, j0, j1):
+            nc.vector.reciprocal(out=vcur[b][:, j0:j1], in_=src[:, j0:j1])
             with nc.allow_low_precision(reason="the bf16 head of v; its tail goes into the second column"):
-                nc.vector.reciprocal(out=vsp[b][:, :, 0], in_=src[:])
-            nc.vector.tensor_tensor(out=vsp[b][:, :, 1], in0=vcur[b][:], in1=vsp[b][:, :, 0],
+                nc.vector.reciprocal(out=vsp[b][:, j0:j1, 0], in_=src[:, j0:j1])
+
+        def v_lo(b, j0, j1):
+            nc.vector.tensor_tensor(out=vsp[b][:, j0:j1, 1], in0=vcur[b][:, j0:j1], in1=vsp[b][:, j0:j1, 0],
                                     op=ALU.subtract)
-            Rt[b] = psum.tile([P, 8, 2], F32, name="R", tag="mv%d" % b, bufs=1)
-            nc.tensor.matmul(out=Rt[b][:].rearrange("p i s -> p (i s)"), lhsT=ident_bf[:], rhs=zeros[:],
+
+        def v_new(b):
+            vcur[b] = small.tile([P, 8], F32, name="v%d" % b, tag="v%d" % b)
+            vsp[b] = small.tile([P, 8, 2], BF16, name="vsp%d" % b, tag="vsp%d" % b)
+
+        def v_red(b, j0, j1):
+            nc.vector.tensor_reduce(out=sums[b][:, j0:j1], in_=halves[b][:, j0:j1, :], axis=AX.X, op=ALU.add)
+
+        def g_open(b):
+            bank[b] = psum.tile([P, 8, 2], F32, name="R", tag="mv%d" % b, bufs=1)
+            nc.tensor.matmul(out=bank[b][:].rearrange("p i s -> p (i s)"), lhsT=ident_bf[:], rhs=zeros[:],
                              start=True, stop=False)
-            for cj in range(8):
+
+        def g_tiles(b, j0, j1):
+            for cj in range(j0, j1):
                 for s, piece in enumerate((TH[b], TL[b])):
                     for i in range(8):
-                        nc.tensor.matmul(out=Rt[b][:, i, :], lhsT=piece[:, cj, P * i:P * i + P],
-                                         rhs=vsp[b][:, col(cj), :],
+                        nc.tensor.matmul(out=bank[b][:, i, :], lhsT=piece[:, cj, P * i:P * i + P],
+                                         rhs=vsp[b][:, cj, :],
                                          start=False, stop=(cj == 7 and s == 1 and i == 7))
 
-        rcur = [None, None]
-
-        def r_of(b):
+        def u_red(b):
             rcur[b] = small.tile([P, 8], F32, name="r%d" % b, tag="r%d" % b)
-            nc.vector.tensor_reduce(out=rcur[b][:], in_=Rt[b][:], axis=AX.X, op=ALU.add)
+            nc.vector.tensor_reduce(out=rcur[b][:], in_=bank[b][:], axis=AX.X, op=ALU.add)
 
-        def u_of(b):
-            u = small.tile([P, 8], F32, name="u%d" % b, tag="u%d" % b)
-            nc.vector.reciprocal(out=u[:], in_=rcur[b][:])
+        def u_rec(b):
+            ucur[b] = small.tile([P, 8], F32, name="u%d" % b, tag="u%d" % b)
+            nc.vector.reciprocal(out=ucur[b][:], in_=rcur[b][:])
             for hh in range(2):
-                ub[b][hh] = spread_half(u, hh, "ub%d" % b)
+                ub[b][hh] = spread_half(ucur[b], hh, "qk", 4)
 
         def f_side(b):
+            if ubs[0] is None:
+                ubs[0] = big.tile([P, B, T], F32, name="ubs", tag="sA", align_bytes=64)
             for hh in range(2):
-                nc.scalar.copy(out=ubs[:, b, 512 * hh:512 * hh + 512], in_=ub[b][hh][:])
+                nc.scalar.copy(out=ubs[0][:, b, 512 * hh:512 * hh + 512], in_=ub[b][hh][:])
             for cj in range(NV, 8):
                 prod = scr.tile([P, T], F32, name="prod", tag="prod", bufs=2)
-                nc.gpsimd.tensor_tensor(out=prod[:], in0=F[b][:, cj, :], in1=ubs[:, b, :], op=ALU.mult)
+                nc.gpsimd.tensor_tensor(out=prod[:], in0=F[b][:, cj, :], in1=ubs[0][:, b, :], op=ALU.mult)
                 nc.scalar.activation(out=prod[:], in_=prod[:], func=ACT.Copy,
-                                     accum_out=sums[b][:, col(cj):col(cj) + 1])
+                                     accum_out=sums[b][:, cj:cj + 1])
 
-        def f_update(b, step):
-            halves[b] = small.tile([P, NV, 2], F32, name="halves%d" % b, tag="halves%d" % b)
-            for cj in range(NV):
-                for hh in range(2):
-                    if 2 * cj + hh == 2 * NV - 2:
-                        r_of(1 - b)
-                    if 2 * cj + hh == 2 * NV - 2 + 1:
-                        u_of(1 - b)
-                        if step < 7:
-                            f_side(1 - b)
-                        vp_eighth(step)
-                    junk = scr.tile([P, 512], F32, name="junk", tag="junk", bufs=4)
-                    nc.vector.scalar_tensor_tensor(
-                        out=junk[:], in0=F[b][:, cj, 512 * hh:512 * hh + 512], scalar=1.0,
-                        in1=ub[b][hh][:], op0=ALU.mult, op1=ALU.mult,
-                        accum_out=halves[b][:, cj, hh:hh + 1])
-            nc.vector.tensor_reduce(out=sums[b][:, 0:NV], in_=halves[b][:], axis=AX.X, op=ALU.add)
+        def f_vec(b, k):
+            cj, hh = k // 2, k % 2
+            if k == 0:
+                halves[b] = small.tile([P, NV, 2], F32, name="halves%d" % b, tag="halves%d" % b)
+            junk = scr.tile([P, 512], F32, name="junk", tag="junk", bufs=3)
+            nc.vector.scalar_tensor_tensor(
+                out=junk[:], in0=F[b][:, cj, 512 * hh:512 * hh + 512], scalar=1.0,
+                in1=ub[b][hh][:], op0=ALU.mult, op1=ALU.mult,
+                accum_out=halves[b][:, cj, hh:hh + 1])
 
         wc = const.tile([P, D], U32, name="wc", align_bytes=64)
         ws = const.tile([P, D], U8, name="ws", align_bytes=64)
@@ -230,29 +263,24 @@ def tile_sinkhornattention_pa_kernel(tc, q_proj, k_proj, v, w_v, out):
         vpg = [None, None]
 
         def v_load(b):
-            v_raw[b] = big.tile([P, 8, D], BF16, name="v_raw%d" % b, tag=("sA", "sD")[b], align_bytes=64)
+            v_raw[b] = big.tile([P, 8, D], BF16, name="v_raw%d" % b, tag=("sA", "sE")[b], align_bytes=64)
             nc.sync.dma_start(out=v_raw[b][:].rearrange("p (c j) d -> p c j d", c=2),
                               in_=v[b].rearrange("(c p j) d -> p c j d", c=2, j=4))
 
-        def w_quant():
-            nc.vector.tensor_copy(out=wg[:], in_=w_raw[:].rearrange("p t c -> p c t"))
-            nc.vector.quantize_mx(out=wc[:].bitcast(FP8X4), scales=ws[:],
-                                  in_=wg[:].rearrange("p c t -> p (c t)"))
-
-        def v_tr(b):
+        def v_tr(b, g):
             vw = v_raw[b][:].bitcast(F32)
-            vg[b] = big.tile([P, N, 4], BF16, name="vg", tag=("sB", "sC")[b], align_bytes=64)
+            if g == 0:
+                vg[b] = big.tile([P, N, 4], BF16, name="vg", tag=("sY", "sC")[b], align_bytes=64)
             vgw = vg[b][:].bitcast(F32)
-            for g in range(4):
-                pv = psum.tile([P, 2, 2, P], F32, name="pv", tag="tr", bufs=2)
-                for a in range(2):
-                    for u in range(2):
-                        nc.tensor.transpose(out=pv[:, a, u, :],
-                                            in_=vw[:, 2 * g + a, P * u:P * u + P],
-                                            identity=ident_f[:])
-                nc.vector.tensor_copy(
-                    out=vgw[:, 256 * g:256 * g + 256, :].rearrange("p (a n) u -> p a n u", a=2),
-                    in_=pv[:].rearrange("p a u n -> p a n u"))
+            pv = psum.tile([P, 2, 2, P], F32, name="pv", tag="tr", bufs=2)
+            for a in range(2):
+                for u in range(2):
+                    nc.tensor.transpose(out=pv[:, a, u, :],
+                                        in_=vw[:, 2 * g + a, P * u:P * u + P],
+                                        identity=ident_f[:])
+            nc.scalar.copy(
+                out=vgw[:, 256 * g:256 * g + 256, :].rearrange("p (a n) u -> p a n u", a=2),
+                in_=pv[:].rearrange("p a u n -> p a n u"))
 
         def v_quant(b):
             vc[b] = big.tile([P, N], U32, name="vc", tag="vc%d" % b, align_bytes=64)
@@ -260,24 +288,22 @@ def tile_sinkhornattention_pa_kernel(tc, q_proj, k_proj, v, w_v, out):
             nc.vector.quantize_mx(out=vc[b][:].bitcast(FP8X4), scales=vs_[b][:],
                                   in_=vg[b][:].rearrange("p n t -> p (n t)"))
 
-        def vp_eighth(step):
-            b = step // 4
-            c = (step % 4) // 2
-            if step % 4 == 0:
-                vpg[b] = big.tile([P, 2, D, 4], BF16, name="vpg", tag=("sE", "sF")[b], align_bytes=64)
-            for eq in (2 * (step % 2), 2 * (step % 2) + 1):
-                pvp = psum.tile([P, 4, P], F32, name="pvp", tag="tr", bufs=2)
-                for j in range(4):
-                    cj = 4 * c + j
-                    nc.tensor.matmul_mx(
-                        out=pvp[:, j, :],
-                        lhsT=vc[b][:, P * cj:P * cj + P].bitcast(FP8X4),
-                        lhsT_scale=vs_[b][:, P * cj:P * cj + P],
-                        rhs=wc[:, P * eq:P * eq + P].bitcast(FP8X4),
-                        rhs_scale=ws[:, P * eq:P * eq + P],
-                        start=True, stop=True)
-                nc.scalar.copy(out=vpg[b][:, c, P * eq:P * eq + P, :],
-                               in_=pvp[:].rearrange("p j e -> p e j"))
+        def vp_piece(b, k):
+            c, eq = k // 4, k % 4
+            if k == 0:
+                vpg[b] = big.tile([P, 2, D, 4], BF16, name="vpg", tag=("sD", "sF")[b], align_bytes=64)
+            pvp = psum.tile([P, 4, P], F32, name="pvp", tag="tr", bufs=2)
+            for j in range(4):
+                cj = 4 * c + j
+                nc.tensor.matmul_mx(
+                    out=pvp[:, j, :],
+                    lhsT=vc[b][:, P * cj:P * cj + P].bitcast(FP8X4),
+                    lhsT_scale=vs_[b][:, P * cj:P * cj + P],
+                    rhs=wc[:, P * eq:P * eq + P].bitcast(FP8X4),
+                    rhs_scale=ws[:, P * eq:P * eq + P],
+                    start=True, stop=True)
+            nc.scalar.copy(out=vpg[b][:, c, P * eq:P * eq + P, :],
+                           in_=pvp[:].rearrange("p j e -> p e j"))
 
         def vp_quant(b):
             nc.vector.quantize_mx(out=vpc[b][:].rearrange("p c e -> p (c e)").bitcast(FP8X4),
@@ -289,123 +315,170 @@ def tile_sinkhornattention_pa_kernel(tc, q_proj, k_proj, v, w_v, out):
             q_tr(i)
         for cj in range(4):
             k_tr(0, cj)
-        q2_spread(0)
-        for cj in range(4):
             k_norm(0, cj)
+        q2_spread(0)
+        for i in range(4, 8):
+            q_norm(i)
         mm(0, 0, 0)
         mm(0, 1, 0)
         for i in range(4, 8):
-            q_norm(i)
             q_tr(i)
         v_load(0)
         mm(0, 2, 0)
         mm(0, 3, 0)
         q2_spread(1)
         for cj in range(4, 8):
-            k_tr(0, cj)
             k_norm(0, cj)
+        for cj in range(8):
+            k_norm(1, cj)
         for cj in range(4):
             mm(0, cj, 1)
+            k_tr(0, 4 + cj)
             if cj > 0:
                 clamp(0, cj - 1)
                 sqrt_(0, cj - 1)
-            k_norm(1, cj)
+        w_raw = big.tile([P, 4, D], BF16, name="w_raw", tag="sB", align_bytes=64)
+        nc.sync.dma_start(out=w_raw[:].rearrange("p (u e) c -> p u e c", u=2),
+                          in_=w_v.rearrange("(u q e) c -> q u e c", u=2, e=2))
+        wg = big.tile([P, D, 4], BF16, name="wg", tag="sX", align_bytes=64)
+        nc.gpsimd.tensor_scalar(out=wg[:], in0=w_raw[:].rearrange("p t c -> p c t"), scalar1=1.0,
+                                scalar2=0.0, op0=ALU.mult, op1=ALU.add)
+        floors(0)
         for cj in range(4, 8):
             mm(0, cj, 0)
             clamp(0, cj - 1)
             sqrt_(0, cj - 1)
             mm(0, cj, 1)
-            k_tr(1, 2 * (cj - 4))
-            k_tr(1, 2 * (cj - 4) + 1)
-            k_norm(1, cj)
+            if cj >= 6:
+                k_tr(1, 2 * (cj - 6))
+                k_tr(1, 2 * (cj - 6) + 1)
+            v_tr(0, cj - 4)
         clamp(0, 7)
         sqrt_(0, 7)
         min_sqrt(0)
+        v_load(1)
+
         for cj in range(8):
             expo(0, cj)
+        floors(1)
+        v_quant(0)
+        nc.vector.quantize_mx(out=wc[:].bitcast(FP8X4), scales=ws[:],
+                              in_=wg[:].rearrange("p c t -> p (c t)"))
+        for cj in range(8):
             mm(1, cj, 0)
             if cj > 0:
                 clamp(1, cj - 1)
-            if cj > 0:
-                hi(0, cj - 1)
-                lo_gpsimd(0, cj - 1)
+                sqrt_(1, cj - 1)
+            if cj < 4:
+                k_tr(1, 4 + cj)
             mm(1, cj, 1)
+            if cj < SPLIT_GPSIMD:
+                hilo_gpsimd(0, cj)
         clamp(1, 7)
-        hi(0, 7)
-        lo_gpsimd(0, 7)
-        for cj in range(8):
-            sqrt_(1, cj)
+        sqrt_(1, 7)
         min_sqrt(1)
+        for cj in range(SPLIT_GPSIMD, 8):
+            hi(0, cj)
+            if cj > SPLIT_GPSIMD:
+                lo(0, cj - 1)
+        lo(0, 7)
+        v_first(0)
         for cj in range(8):
             expo(1, cj)
-        w_raw = big.tile([P, 4, D], BF16, name="w_raw", tag="sG", align_bytes=64)
-        nc.sync.dma_start(out=w_raw[:].rearrange("p (u e) c -> p u e c", u=2),
-                          in_=w_v.rearrange("(u q e) c -> q u e c", u=2, e=2))
-        wg = big.tile([P, D, 4], BF16, name="wg", tag="sE", align_bytes=64)
-        v_load(1)
-        v_tr(0)
-        ubs = big.tile([P, B, T], F32, name="ubs", tag="sA", align_bytes=64)
-        g_update(0, first[0])
-        w_quant()
-        v_quant(0)
-        for cj in range(8):
+        g_open(0)
+        g_tiles(0, 0, 8)
+        for k in range(8):
+            vp_piece(0, k)
+        for cj in range(7):
             hi(1, cj)
-            if cj == 5:
-                r_of(0)
-            if cj < 5:
-                lo_gpsimd(1, cj)
-            if cj > 5:
+            if cj > 0:
                 lo(1, cj - 1)
-            if cj == 5:
-                u_of(0)
-                f_side(0)
+        hi(1, 7)
+        u_red(0)
+        lo(1, 6)
+        u_rec(0)
+        f_side(0)
         lo(1, 7)
-        v_tr(1)
-        g_update(1, first[1])
-        v_quant(1)
+        v_first(1)
+        g_open(1)
+        g_tiles(1, 0, 8)
+        for g in range(4):
+            v_tr(1, g)
 
         def w_scale(b):
             for cj in range(8):
                 if cj % 2 == 0:
                     nc.scalar.activation(out=F[b][:, cj, :], in_=F[b][:, cj, :], func=ACT.Copy,
-                                         scale=vcur[b][:, col(cj):col(cj) + 1])
+                                         scale=vcur[b][:, cj:cj + 1])
                 else:
                     nc.gpsimd.tensor_scalar(out=F[b][:, cj, :], in0=F[b][:, cj, :],
-                                            scalar1=vcur[b][:, col(cj):col(cj) + 1], scalar2=0.0,
+                                            scalar1=vcur[b][:, cj:cj + 1], scalar2=0.0,
                                             op0=ALU.mult, op1=ALU.add)
 
-        for it in range(ITERS - 1):
-            for b in range(B):
-                f_update(b, 2 * it + b)
-                g_update(b, sums[b])
-                if it == 2 and b == 0:
-                    vp_quant(0)
-                if it == ITERS - 2:
-                    w_scale(b)
+        vp_todo = list(range(8))
 
-        pis = [const.tile([P, 2, T], U8, name="pis%d" % b, align_bytes=64) for b in range(B)]
+        def slot(x, y, step):
+            for k in range(2 * NV):
+                f_vec(x, k)
+                if step > 0:
+                    if k == 0:
+                        v_red(y, EARLY, NV)
+                    if k == 1:
+                        v_rec(y, sums[y], EARLY, 8)
+                    if k == 2:
+                        v_lo(y, EARLY, 8)
+                        g_tiles(y, EARLY, 8)
+                        if step > 2:
+                            vp_piece(1, vp_todo.pop(0))
+                        if step == STEPS - 1:
+                            w_scale(y)
+                if k == 5 and step == 2:
+                    v_quant(1)
+                if k == 7:
+                    u_red(y)
+                if k == 8:
+                    u_rec(y)
+                    if step < STEPS - 1:
+                        f_side(y)
+                    v_new(x)
+                    v_red(x, 0, EARLY)
+                if k == 9:
+                    v_rec(x, sums[x], 0, EARLY)
+                    v_lo(x, 0, EARLY)
+                    g_open(x)
+                    g_tiles(x, 0, EARLY)
+
+        for step in range(STEPS):
+            slot(step % 2, 1 - step % 2, step)
+        v_red(1, EARLY, NV)
+        v_rec(1, sums[1], EARLY, 8)
+        v_lo(1, EARLY, 8)
+        g_tiles(1, EARLY, 8)
+        w_scale(1)
+
+        pis = big.tile([P, B, 2, T], U8, name="pis", tag="sG", align_bytes=64)
         pig = [big.tile([P, 2, T, 4], BF16, name="pig%d" % b, tag="th%d" % b, align_bytes=64) for b in range(B)]
         pic = [big.tile([P, 2, T], U32, name="pic%d" % b, tag="tl%d" % b, align_bytes=64) for b in range(B)]
 
-        def pi_mul(b, h):
+        def pi_mul(b, h, c):
             sl = slice(512 * h, 512 * h + 512)
-            for c in range(2):
-                nc.vector.tensor_tensor(
-                    out=pig[b][:, c, sl, :].rearrange("p (g i) j -> p g j i", i=4),
-                    in0=F[b][:, 4 * c:4 * c + 4, sl].rearrange("p j (g i) -> p g j i", i=4),
-                    in1=ub[b][h][:].rearrange("p (g i) -> p g i", i=4).unsqueeze(2).to_broadcast([P, 128, 4, 4]),
-                    op=ALU.mult)
+            nc.vector.tensor_tensor(
+                out=pig[b][:, c, sl, :].rearrange("p (g i) j -> p g j i", i=4),
+                in0=F[b][:, 4 * c:4 * c + 4, sl].rearrange("p j (g i) -> p g j i", i=4),
+                in1=ub[b][h][:].rearrange("p (g i) -> p g i", i=4).unsqueeze(2).to_broadcast([P, 128, 4, 4]),
+                op=ALU.mult)
 
         def pi_quant(b, h):
             sl = slice(512 * h, 512 * h + 512)
             for c in range(2):
-                nc.vector.quantize_mx(out=pic[b][:, c, sl].bitcast(FP8X4), scales=pis[b][:, c, sl],
+                nc.vector.quantize_mx(out=pic[b][:, c, sl].bitcast(FP8X4), scales=pis[:, b, c, sl],
                                       in_=pig[b][:, c, sl, :].rearrange("p t j -> p (t j)"))
 
         def out_half(b, h):
             ov = out[b].rearrange("(p i) d -> p i d", i=8)
+            last = b == 1 and h == 1
             for a2 in range(2):
-                ost = big.tile([P, 2, D], F32, name="ost", tag=("sB", "sC", "sE", "sF")[2 * h + a2],
+                ost = big.tile([P, 2, D], F32, name="ost", tag=("sA", "sE", "sB", "sC")[2 * h + a2],
                                align_bytes=64)
                 for a in range(2):
                     i = 4 * h + 2 * a2 + a
@@ -414,24 +487,39 @@ def tile_sinkhornattention_pa_kernel(tc, q_proj, k_proj, v, w_v, out):
                         nc.tensor.matmul_mx(
                             out=po[:],
                             lhsT=pic[b][:, c, P * i:P * i + P].bitcast(FP8X4),
-                            lhsT_scale=pis[b][:, c, P * i:P * i + P],
+                            lhsT_scale=pis[:, b, c, P * i:P * i + P],
                             rhs=vpc[b][:, c, :].bitcast(FP8X4),
                             rhs_scale=vps[b][:, c, :],
                             start=(c == 0), stop=(c == 1))
-                    nc.scalar.copy(out=ost[:, a, :], in_=po[:])
+                    if last and a == 1:
+                        nc.vector.tensor_copy(out=ost[:, a, :], in_=po[:])
+                    else:
+                        nc.scalar.copy(out=ost[:, a, :], in_=po[:])
+                    if last:
+                        nc.sync.dma_start(out=ov[:, i, :], in_=ost[:, a, :])
                 i0 = 4 * h + 2 * a2
-                nc.sync.dma_start(out=ov[:, i0:i0 + 2, :], in_=ost[:])
+                if not last:
+                    nc.sync.dma_start(out=ov[:, i0:i0 + 2, :], in_=ost[:])
 
-        pi_mul(0, 0)
-        vp_quant(1)
+        while vp_todo:
+            vp_piece(1, vp_todo.pop(0))
+        pi_mul(0, 0, 0)
+        pi_mul(0, 0, 1)
+        vp_quant(0)
         pi_quant(0, 0)
+        u_red(1)
+        pi_mul(0, 1, 0)
+        u_rec(1)
         out_half(0, 0)
-        r_of(1)
-        pi_mul(0, 1)
-        u_of(1)
+        pi_mul(0, 1, 1)
         pi_quant(0, 1)
+        pi_mul(1, 0, 0)
+        pi_mul(1, 0, 1)
         out_half(0, 1)
-        for h in range(2):
-            pi_mul(1, h)
-            pi_quant(1, h)
-            out_half(1, h)
+        vp_quant(1)
+        pi_quant(1, 0)
+        out_half(1, 0)
+        pi_mul(1, 1, 0)
+        pi_mul(1, 1, 1)
+        pi_quant(1, 1)
+        out_half(1, 1)

@@ -26,7 +26,22 @@ QA = (2, 1)
 SPLIT_GPSIMD = 5
 NV = 6
 EARLY = 4
+GHL1 = (0, 3, 5)
+SHI1 = ()
 STEPS = 2 * (ITERS - 1)
+K0 = 0
+VA = 0
+D0 = 0
+D1 = 0
+D2 = 0
+D3 = 0
+PGA = ()
+PG1 = ()
+WS1 = (0, 1, 2, 4, 6)
+WG1 = (3, 5, 7)
+KU = 7
+KV = 8
+KQ = 5
 
 
 def tile_sinkhornattention_pa_kernel(tc, q_proj, k_proj, v, w_v, out):
@@ -45,6 +60,12 @@ def tile_sinkhornattention_pa_kernel(tc, q_proj, k_proj, v, w_v, out):
         make_identity(nc, ident_f[:])
         zeros = const.tile([P, 16], BF16, name="zeros")
         nc.vector.memset(zeros[:], 0.0)
+
+        wide = const.tile([P, 512], BF16, name="wide")
+        nc.vector.memset(wide[:], 0.0)
+        dump = psum.tile([P, 512], F32, name="dump", tag="tr", bufs=2)
+        for n in range(5):
+            nc.tensor.matmul(out=dump[:], lhsT=ident_bf[:], rhs=wide[:], start=True, stop=True)
 
         q_raw = big.tile([P, 8, D], BF16, name="q_raw", tag="sA", align_bytes=64)
         k_raw = [big.tile([P, 8, D], BF16, name="k_raw%d" % b, tag=("sB", "sC")[b], align_bytes=64)
@@ -164,10 +185,12 @@ def tile_sinkhornattention_pa_kernel(tc, q_proj, k_proj, v, w_v, out):
                 nc.scalar.activation(out=F[b][:, cj, :], in_=F[b][:, cj, :], func=ACT.Sqrt)
 
         def min_sqrt(b):
-            sl = slice(8 - QA[b], 8)
-            nc.vector.tensor_reduce(out=minsq[b][:, sl], in_=minh[b][:, sl, :], axis=AX.X, op=ALU.min)
-            nc.vector.tensor_tensor(out=minsq[b][:, sl], in0=minsq[b][:, sl], in1=k2[b][:, sl], op=ALU.add)
-            nc.scalar.activation(out=mn[b][:], in_=minsq[b][:], func=ACT.Sqrt)
+            n = 8 - QA[b]
+            nc.vector.tensor_reduce(out=minsq[b][:, n:8], in_=minh[b][:, n:8, :], axis=AX.X, op=ALU.min)
+            nc.scalar.activation(out=mn[b][:, 0:n], in_=minsq[b][:, 0:n], func=ACT.Sqrt)
+            for cj in range(n, 8):
+                nc.scalar.activation(out=mn[b][:, cj:cj + 1], in_=minsq[b][:, cj:cj + 1], func=ACT.Sqrt,
+                                     bias=k2[b][:, cj:cj + 1])
 
         def expo(b, cj):
             nc.scalar.activation(out=F[b][:, cj, :], in_=F[b][:, cj, :], func=ACT.Exp,
@@ -188,8 +211,7 @@ def tile_sinkhornattention_pa_kernel(tc, q_proj, k_proj, v, w_v, out):
                                     op=ALU.subtract)
 
         def v_first(b):
-            vcur[b] = small.tile([P, 8], F32, name="v%d" % b, tag="v%d" % b)
-            vsp[b] = small.tile([P, 8, 2], BF16, name="vsp%d" % b, tag="vsp%d" % b)
+            v_new(b)
             v_rec(b, first[b], 0, 8)
             v_lo(b, 0, 8)
 
@@ -210,21 +232,26 @@ def tile_sinkhornattention_pa_kernel(tc, q_proj, k_proj, v, w_v, out):
             nc.vector.tensor_reduce(out=sums[b][:, j0:j1], in_=halves[b][:, j0:j1, :], axis=AX.X, op=ALU.add)
 
         def g_open(b):
-            bank[b] = psum.tile([P, 8, 2], F32, name="R", tag="mv%d" % b, bufs=1)
-            nc.tensor.matmul(out=bank[b][:].rearrange("p i s -> p (i s)"), lhsT=ident_bf[:], rhs=zeros[:],
-                             start=True, stop=False)
+            bank[b] = psum.tile([P, 512], F32, name="R", tag="mv%d" % b, bufs=1)
+            nc.tensor.matmul(out=bank[b][:, 0:16], lhsT=ident_bf[:], rhs=zeros[:], start=True, stop=False)
+
+        def keep_clock(b, passes):
+            for n in range(passes):
+                nc.tensor.matmul_mx(out=bank[b][:], lhsT=vc[0][:, 0:P].bitcast(FP8X4), lhsT_scale=vs_[0][:, 0:P],
+                                    rhs=wc[:].bitcast(FP8X4), rhs_scale=ws[:], start=True, stop=True)
 
         def g_tiles(b, j0, j1):
             for cj in range(j0, j1):
                 for s, piece in enumerate((TH[b], TL[b])):
                     for i in range(8):
-                        nc.tensor.matmul(out=bank[b][:, i, :], lhsT=piece[:, cj, P * i:P * i + P],
+                        nc.tensor.matmul(out=bank[b][:, 2 * i:2 * i + 2], lhsT=piece[:, cj, P * i:P * i + P],
                                          rhs=vsp[b][:, cj, :],
                                          start=False, stop=(cj == 7 and s == 1 and i == 7))
 
         def u_red(b):
             rcur[b] = small.tile([P, 8], F32, name="r%d" % b, tag="r%d" % b)
-            nc.vector.tensor_reduce(out=rcur[b][:], in_=bank[b][:], axis=AX.X, op=ALU.add)
+            nc.vector.tensor_reduce(out=rcur[b][:], in_=bank[b][:, 0:16].rearrange("p (i k) -> p i k", k=2), axis=AX.X,
+                                    op=ALU.add)
 
         def u_rec(b):
             ucur[b] = small.tile([P, 8], F32, name="u%d" % b, tag="u%d" % b)
@@ -232,11 +259,13 @@ def tile_sinkhornattention_pa_kernel(tc, q_proj, k_proj, v, w_v, out):
             for hh in range(2):
                 ub[b][hh] = spread_half(ucur[b], hh, "qk", 4)
 
-        def f_side(b):
+        def u_copy(b, hh):
             if ubs[0] is None:
-                ubs[0] = big.tile([P, B, T], F32, name="ubs", tag="sA", align_bytes=64)
-            for hh in range(2):
+                ubs[0] = big.tile([P, B, T], F32, name="ubs", tag="sY", align_bytes=64)
+            if True:
                 nc.scalar.copy(out=ubs[0][:, b, 512 * hh:512 * hh + 512], in_=ub[b][hh][:])
+
+        def f_side(b):
             for cj in range(NV, 8):
                 prod = scr.tile([P, T], F32, name="prod", tag="prod", bufs=2)
                 nc.gpsimd.tensor_tensor(out=prod[:], in0=F[b][:, cj, :], in1=ubs[0][:, b, :], op=ALU.mult)
@@ -387,78 +416,109 @@ def tile_sinkhornattention_pa_kernel(tc, q_proj, k_proj, v, w_v, out):
             expo(1, cj)
         g_open(0)
         g_tiles(0, 0, 8)
-        for k in range(8):
-            vp_piece(0, k)
-        for cj in range(7):
-            hi(1, cj)
-            if cj > 0:
-                lo(1, cj - 1)
-        hi(1, 7)
-        u_red(0)
-        lo(1, 6)
-        u_rec(0)
-        f_side(0)
-        lo(1, 7)
+        for cj in GHL1:
+            hilo_gpsimd(1, cj)
+        for cj in SHI1:
+            nc.scalar.copy(out=TH[1][:, cj, :], in_=F[1][:, cj, :])
+        ops = []
+        wait = []
+        for cj in range(8):
+            if cj not in GHL1:
+                if cj not in SHI1:
+                    ops.append(lambda cj=cj: hi(1, cj))
+                if wait:
+                    ops.append(wait.pop(0))
+                wait.append(lambda cj=cj: lo(1, cj))
+        ops.extend(wait)
+        for n, op in enumerate(ops):
+            if n == len(ops) - 3:
+                u_red(0)
+            if n == len(ops) - 2:
+                u_rec(0)
+            op()
         v_first(1)
+        keep_clock(0, K0)
         g_open(1)
-        g_tiles(1, 0, 8)
-        for g in range(4):
-            v_tr(1, g)
+        for cj in range(8):
+            g_tiles(1, cj, cj + 1)
+            if cj in PG1:
+                keep_clock(0, 1)
 
-        def w_scale(b):
-            for cj in range(8):
-                if cj % 2 == 0:
-                    nc.scalar.activation(out=F[b][:, cj, :], in_=F[b][:, cj, :], func=ACT.Copy,
-                                         scale=vcur[b][:, cj:cj + 1])
-                else:
-                    nc.gpsimd.tensor_scalar(out=F[b][:, cj, :], in0=F[b][:, cj, :],
-                                            scalar1=vcur[b][:, cj:cj + 1], scalar2=0.0,
-                                            op0=ALU.mult, op1=ALU.add)
+        def w_scalar(b, tiles):
+            for cj in tiles:
+                nc.scalar.activation(out=F[b][:, cj, :], in_=F[b][:, cj, :], func=ACT.Copy,
+                                     scale=vcur[b][:, cj:cj + 1])
 
-        vp_todo = list(range(8))
+        def w_gpsimd(b, tiles):
+            for cj in tiles:
+                nc.gpsimd.tensor_scalar(out=F[b][:, cj, :], in0=F[b][:, cj, :],
+                                        scalar1=vcur[b][:, cj:cj + 1], scalar2=0.0,
+                                        op0=ALU.mult, op1=ALU.add)
+
+        vp_todo = list(range(16))
+
+        def late(b):
+            for cj in range(EARLY, 8):
+                g_tiles(b, cj, cj + 1)
+                if cj in PGA:
+                    keep_clock(1 - b, 1)
 
         def slot(x, y, step):
+            last = step == STEPS - 1
             for k in range(2 * NV):
                 f_vec(x, k)
+                if k < 2:
+                    u_copy(x, k)
+                if k == 1 and step > 0:
+                    v_rec(y, sums[y], EARLY, 8)
+                if k == 1:
+                    if last:
+                        w_scalar(y, (0, 1, 2))
+                    if step < 2:
+                        v_tr(1, 2 * step)
+                        v_tr(1, 2 * step + 1)
+                    if not last:
+                        for n in range(2):
+                            e = vp_todo.pop(0)
+                            vp_piece(e // 8, e % 8)
+                    f_side(x)
                 if step > 0:
                     if k == 0:
                         v_red(y, EARLY, NV)
-                    if k == 1:
-                        v_rec(y, sums[y], EARLY, 8)
                     if k == 2:
                         v_lo(y, EARLY, 8)
-                        g_tiles(y, EARLY, 8)
-                        if step > 2:
-                            vp_piece(1, vp_todo.pop(0))
-                        if step == STEPS - 1:
-                            w_scale(y)
-                if k == 5 and step == 2:
+                        late(y)
+                        keep_clock(x, D2)
+                if k == KQ and step == 3:
                     v_quant(1)
-                if k == 7:
+                if k == KU:
                     u_red(y)
-                if k == 8:
+                if k == KU + 1:
                     u_rec(y)
-                    if step < STEPS - 1:
-                        f_side(y)
+                if k == KV:
                     v_new(x)
                     v_red(x, 0, EARLY)
-                if k == 9:
+                if k == KV + 1:
                     v_rec(x, sums[x], 0, EARLY)
                     v_lo(x, 0, EARLY)
+                    keep_clock(y, D0)
                     g_open(x)
-                    g_tiles(x, 0, EARLY)
+                    for cj in range(EARLY):
+                        g_tiles(x, cj, cj + 1)
+                        if cj in PGA:
+                            keep_clock(y, 1)
+                    keep_clock(y, D1)
 
         for step in range(STEPS):
             slot(step % 2, 1 - step % 2, step)
-        v_red(1, EARLY, NV)
-        v_rec(1, sums[1], EARLY, 8)
-        v_lo(1, EARLY, 8)
-        g_tiles(1, EARLY, 8)
-        w_scale(1)
 
         pis = big.tile([P, B, 2, T], U8, name="pis", tag="sG", align_bytes=64)
-        pig = [big.tile([P, 2, T, 4], BF16, name="pig%d" % b, tag="th%d" % b, align_bytes=64) for b in range(B)]
-        pic = [big.tile([P, 2, T], U32, name="pic%d" % b, tag="tl%d" % b, align_bytes=64) for b in range(B)]
+        pig = [None, None]
+        pic = [None, None]
+
+        def pi_tiles(b):
+            pig[b] = big.tile([P, 2, T, 4], BF16, name="pig", tag="th%d" % b, align_bytes=64)
+            pic[b] = big.tile([P, 2, T], U32, name="pic", tag="tl%d" % b, align_bytes=64)
 
         def pi_mul(b, h, c):
             sl = slice(512 * h, 512 * h + 512)
@@ -468,9 +528,19 @@ def tile_sinkhornattention_pa_kernel(tc, q_proj, k_proj, v, w_v, out):
                 in1=ub[b][h][:].rearrange("p (g i) -> p g i", i=4).unsqueeze(2).to_broadcast([P, 128, 4, 4]),
                 op=ALU.mult)
 
-        def pi_quant(b, h):
+        def pi_mul_gpsimd(b, c, parts):
+            w = 512 // parts
+            for p in range(parts):
+                sl = slice(512 + w * p, 512 + w * p + w)
+                nc.gpsimd.tensor_tensor(
+                    out=pig[b][:, c, sl, :].rearrange("p (g i) j -> p g j i", i=4),
+                    in0=F[b][:, 4 * c:4 * c + 4, sl].rearrange("p j (g i) -> p g j i", i=4),
+                    in1=ubs[0][:, b, sl].rearrange("p (g i) -> p g i", i=4).unsqueeze(2).to_broadcast([P, w // 4, 4, 4]),
+                    op=ALU.mult)
+
+        def pi_quant(b, h, cs=(0, 1)):
             sl = slice(512 * h, 512 * h + 512)
-            for c in range(2):
+            for c in cs:
                 nc.vector.quantize_mx(out=pic[b][:, c, sl].bitcast(FP8X4), scales=pis[:, b, c, sl],
                                       in_=pig[b][:, c, sl, :].rearrange("p t j -> p (t j)"))
 
@@ -501,25 +571,39 @@ def tile_sinkhornattention_pa_kernel(tc, q_proj, k_proj, v, w_v, out):
                 if not last:
                     nc.sync.dma_start(out=ov[:, i0:i0 + 2, :], in_=ost[:])
 
-        while vp_todo:
-            vp_piece(1, vp_todo.pop(0))
+        pi_tiles(0)
+        w_gpsimd(0, (3, 5, 7))
+        nc.scalar.copy(out=ubs[0][:, 0, 512:1024], in_=ub[0][1][:])
+        w_scalar(0, (4, 6))
+        v_red(1, EARLY, NV)
         pi_mul(0, 0, 0)
+        v_rec(1, sums[1], EARLY, 8)
+        v_lo(1, EARLY, 8)
+        late(1)
+        w_scalar(1, WS1)
+        w_gpsimd(1, WG1)
+        while vp_todo:
+            e = vp_todo.pop(0)
+            vp_piece(e // 8, e % 8)
+        pi_tiles(1)
+        pi_mul_gpsimd(0, 1, 2)
         pi_mul(0, 0, 1)
-        vp_quant(0)
-        pi_quant(0, 0)
         u_red(1)
-        pi_mul(0, 1, 0)
+        vp_quant(0)
         u_rec(1)
+        nc.scalar.copy(out=ubs[0][:, 1, 512:1024], in_=ub[1][1][:])
+        pi_mul_gpsimd(1, 1, 2)
+        pi_quant(0, 0)
         out_half(0, 0)
-        pi_mul(0, 1, 1)
-        pi_quant(0, 1)
+        pi_mul(0, 1, 0)
+        pi_quant(0, 1, (0,))
         pi_mul(1, 0, 0)
-        pi_mul(1, 0, 1)
+        pi_quant(0, 1, (1,))
         out_half(0, 1)
+        pi_mul(1, 0, 1)
         vp_quant(1)
         pi_quant(1, 0)
         out_half(1, 0)
         pi_mul(1, 1, 0)
-        pi_mul(1, 1, 1)
         pi_quant(1, 1)
         out_half(1, 1)

@@ -26,8 +26,8 @@ QA = (2, 1)
 SPLIT_GPSIMD = 5
 NV = 6
 EARLY = 4
-GHL1 = (0, 3, 5)
-SHI1 = ()
+GHL1 = ()
+SHI1 = (6, 7)
 STEPS = 2 * (ITERS - 1)
 K0 = 0
 VA = 0
@@ -39,7 +39,7 @@ PGA = ()
 PG1 = ()
 WS1 = (0, 1, 2, 4, 6)
 WG1 = (3, 5, 7)
-KU = 7
+KU = 8
 KV = 8
 KQ = 5
 
@@ -60,12 +60,6 @@ def tile_sinkhornattention_pa_kernel(tc, q_proj, k_proj, v, w_v, out):
         make_identity(nc, ident_f[:])
         zeros = const.tile([P, 16], BF16, name="zeros")
         nc.vector.memset(zeros[:], 0.0)
-
-        wide = const.tile([P, 512], BF16, name="wide")
-        nc.vector.memset(wide[:], 0.0)
-        dump = psum.tile([P, 512], F32, name="dump", tag="tr", bufs=2)
-        for n in range(5):
-            nc.tensor.matmul(out=dump[:], lhsT=ident_bf[:], rhs=wide[:], start=True, stop=True)
 
         q_raw = big.tile([P, 8, D], BF16, name="q_raw", tag="sA", align_bytes=64)
         k_raw = [big.tile([P, 8, D], BF16, name="k_raw%d" % b, tag=("sB", "sC")[b], align_bytes=64)
@@ -420,6 +414,8 @@ def tile_sinkhornattention_pa_kernel(tc, q_proj, k_proj, v, w_v, out):
             hilo_gpsimd(1, cj)
         for cj in SHI1:
             nc.scalar.copy(out=TH[1][:, cj, :], in_=F[1][:, cj, :])
+        for k in range(4):
+            vp_piece(0, k)
         ops = []
         wait = []
         for cj in range(8):
@@ -455,7 +451,7 @@ def tile_sinkhornattention_pa_kernel(tc, q_proj, k_proj, v, w_v, out):
                                         scalar1=vcur[b][:, cj:cj + 1], scalar2=0.0,
                                         op0=ALU.mult, op1=ALU.add)
 
-        vp_todo = list(range(16))
+        vp_todo = list(range(4, 16))
 
         def late(b):
             for cj in range(EARLY, 8):
@@ -478,9 +474,8 @@ def tile_sinkhornattention_pa_kernel(tc, q_proj, k_proj, v, w_v, out):
                         v_tr(1, 2 * step)
                         v_tr(1, 2 * step + 1)
                     if not last:
-                        for n in range(2):
-                            e = vp_todo.pop(0)
-                            vp_piece(e // 8, e % 8)
+                        e = vp_todo.pop(0)
+                        vp_piece(e // 8, e % 8)
                     f_side(x)
                 if step > 0:
                     if k == 0:
@@ -500,6 +495,7 @@ def tile_sinkhornattention_pa_kernel(tc, q_proj, k_proj, v, w_v, out):
                     v_red(x, 0, EARLY)
                 if k == KV + 1:
                     v_rec(x, sums[x], 0, EARLY)
+                if k == KV + 2:
                     v_lo(x, 0, EARLY)
                     keep_clock(y, D0)
                     g_open(x)

from contextlib import ExitStack

import concourse.mybir as mybir
from concourse.masks import make_identity

F32 = mybir.dt.float32
BF16 = mybir.dt.bfloat16
U32 = mybir.dt.uint32
U8 = mybir.dt.uint8
FP8X4 = mybir.dt.float8_e4m3fn_x4
ALU = mybir.AluOpType
ACT = mybir.ActivationFunctionType
AX = mybir.AxisListType

P = 128
B = 2
T = 1024
N = 1024
D = 512
ITERS = 5
TINY = 2.0 ** -90
HAIR = 2.0 ** -22
FLOPS = 2 * B * T * N * D + 2 * B * N * D * D + 2 * B * T * N * D

QA = (2, 1)
SPLIT_GPSIMD = 5
NV = 6
EARLY = 4
GHL1 = ()
SHI1 = (6, 7)
STEPS = 2 * (ITERS - 1)
K0 = 0
VA = 0
D0 = 0
D1 = 0
D2 = 0
D3 = 0
PGA = ()
PG1 = ()
WS1 = (0, 1, 2, 4, 6)
WG1 = (3, 5, 7)
KU = 8
KV = 8
KQ = 5


def tile_sinkhornattention_pa_kernel(tc, q_proj, k_proj, v, w_v, out):
    nc = tc.nc
    with ExitStack() as ctx:
        ctx.enter_context(tc.manual_schedule())
        const = ctx.enter_context(tc.tile_pool(name="const", bufs=1))
        big = ctx.enter_context(tc.tile_pool(name="big", bufs=1))
        scr = ctx.enter_context(tc.tile_pool(name="scr", bufs=2))
        small = ctx.enter_context(tc.tile_pool(name="small", bufs=2))
        psum = ctx.enter_context(tc.psum_pool(name="psum", bufs=1))

        ident_bf = const.tile([P, P], BF16, name="ident_bf")
        make_identity(nc, ident_bf[:])
        ident_f = const.tile([P, P], F32, name="ident_f")
        make_identity(nc, ident_f[:])
        zeros = const.tile([P, 16], BF16, name="zeros")
        nc.vector.memset(zeros[:], 0.0)

        q_raw = big.tile([P, 8, D], BF16, name="q_raw", tag="sA", align_bytes=64)
        k_raw = [big.tile([P, 8, D], BF16, name="k_raw%d" % b, tag=("sB", "sC")[b], align_bytes=64)
                 for b in range(B)]
        v_raw = [None, None]
        qT = big.tile([P, 4, T], BF16, name="qT", tag="sD", align_bytes=64)
        kT = [big.tile([P, 4, N], BF16, name="kT%d" % b, tag=("sE", "sF")[b], align_bytes=64)
              for b in range(B)]
        q2 = const.tile([P, 8], F32, name="q2")
        k2 = [const.tile([P, 8], F32, name="k2_%d" % b) for b in range(B)]
        floor = [const.tile([P, 8], F32, name="floor%d" % b) for b in range(B)]
        minh = [const.tile([P, 8, 2], F32, name="minh%d" % b) for b in range(B)]
        q2b = big.tile([P, T], F32, name="q2b", tag="sG", align_bytes=64)
        F = [big.tile([P, 8, T], F32, name="F%d" % b, tag="F%d" % b) for b in range(B)]
        TH = [big.tile([P, 8, T], BF16, name="TH%d" % b, tag="th%d" % b, align_bytes=64) for b in range(B)]
        TL = [big.tile([P, 8, T], BF16, name="TL%d" % b, tag="tl%d" % b, align_bytes=64) for b in range(B)]
        minsq = [const.tile([P, 8], F32, name="minsq%d" % b) for b in range(B)]
        mn = [const.tile([P, 8], F32, name="mn%d" % b) for b in range(B)]
        sums = [const.tile([P, 8], F32, name="sums%d" % b) for b in range(B)]
        first = [const.tile([P, 8], F32, name="first%d" % b) for b in range(B)]
        bank = [None, None]
        halves = [None, None]
        rcur = [None, None]
        ucur = [None, None]
        ub = [[None, None], [None, None]]
        ubs = [None]
        vcur = [None, None]
        vsp = [None, None]

        qv = q_proj.rearrange("(p i) d -> p i d", i=8)
        kv = [k_proj[b].rearrange("(c p j) d -> p c j d", c=2, j=4) for b in range(B)]
        nc.sync.dma_start(out=q_raw[:, 0:4, :], in_=qv[:, 0:4, :])
        nc.sync.dma_start(out=k_raw[0][:, 0:4, :], in_=kv[0][:, 0, :, :])
        nc.sync.dma_start(out=q_raw[:, 4:8, :], in_=qv[:, 4:8, :])
        nc.sync.dma_start(out=k_raw[0][:, 4:8, :], in_=kv[0][:, 1, :, :])
        nc.sync.dma_start(out=k_raw[1][:, 0:4, :], in_=kv[1][:, 0, :, :])
        nc.sync.dma_start(out=k_raw[1][:, 4:8, :], in_=kv[1][:, 1, :, :])

        def norm(src, dst):
            jn = scr.tile([P, D], BF16, name="jn", tag="jn", bufs=2)
            nc.scalar.activation(out=jn[:], in_=src, func=ACT.Square, accum_out=dst)

        def q_norm(i):
            norm(q_raw[:, i, :], q2[:, i:i + 1])

        def k_norm(b, cj):
            norm(k_raw[b][:, cj, :], k2[b][:, cj:cj + 1])

        def q_tr(i):
            pt = psum.tile([P, 4, P], BF16, name="pt", tag="tr", bufs=2)
            for dk in range(4):
                nc.tensor.transpose(out=pt[:, dk, :], in_=q_raw[:, i, P * dk:P * dk + P],
                                    identity=ident_bf[:])
            nc.vector.tensor_scalar(out=qT[:, :, P * i:P * i + P], in0=pt[:], scalar1=-2.0,
                                    scalar2=None, op0=ALU.mult)

        def k_tr(b, cj):
            pt = psum.tile([P, 4, P], BF16, name="pt", tag="tr", bufs=2)
            for dk in range(4):
                nc.tensor.transpose(out=pt[:, dk, :], in_=k_raw[b][:, cj, P * dk:P * dk + P],
                                    identity=ident_bf[:])
            nc.vector.tensor_copy(out=kT[b][:, :, P * cj:P * cj + P], in_=pt[:])

        def spread_half(vec, hh, tag, bufs):
            pb = psum.tile([P, 512], F32, name="pb", tag=tag, bufs=bufs)
            for a in range(4):
                i = 4 * hh + a
                nc.tensor.transpose(out=pb[:, P * a:P * a + P],
                                    in_=vec[:, i:i + 1].to_broadcast([P, P]),
                                    identity=ident_f[:])
            return pb

        def q2_spread(hh):
            pb = spread_half(q2, hh, "tr", 2)
            nc.vector.tensor_copy(out=q2b[:, 512 * hh:512 * hh + 512], in_=pb[:])

        def added_in_psum(b, cj):
            return cj >= 8 - QA[b]

        def mm(b, cj, h):
            pq = psum.tile([P, 512], F32, name="pq", tag="qk", bufs=4)
            for dk in range(4):
                nc.tensor.matmul(out=pq[:], lhsT=kT[b][:, dk, P * cj:P * cj + P],
                                 rhs=qT[:, dk, 512 * h:512 * h + 512],
                                 start=(dk == 0), stop=(dk == 3 and not added_in_psum(b, cj)))
            if added_in_psum(b, cj):
                for a in range(4):
                    i = 4 * h + a
                    nc.tensor.matmul(out=pq[:, P * a:P * a + P], lhsT=q2[:, i:i + 1].to_broadcast([P, P]),
                                     rhs=ident_f[:], is_transpose=True, start=False, stop=(a == 3))
                nc.vector.tensor_scalar(
                    out=F[b][:, cj, 512 * h:512 * h + 512], in0=pq[:],
                    scalar1=floor[b][:, cj:cj + 1], scalar2=None, op0=ALU.max, op1=ALU.min,
                    accum_out=minh[b][:, cj, h:h + 1])
            else:
                nc.vector.scalar_tensor_tensor(
                    out=F[b][:, cj, 512 * h:512 * h + 512], in0=pq[:],
                    scalar=k2[b][:, cj:cj + 1], in1=q2b[:, 512 * h:512 * h + 512],
                    op0=ALU.add, op1=ALU.add)

        def floors(b):
            nc.vector.tensor_scalar(out=k2[b][:, 4:8], in0=k2[b][:, 4:8], scalar1=TINY, scalar2=None, op0=ALU.max)
            nc.vector.tensor_scalar(out=floor[b][:, 4:8], in0=k2[b][:, 4:8], scalar1=HAIR - 1.0, scalar2=None,
                                    op0=ALU.mult)

        def clamp(b, cj):
            if not added_in_psum(b, cj):
                nc.vector.tensor_scalar(out=F[b][:, cj, :], in0=F[b][:, cj, :], scalar1=TINY,
                                        scalar2=None, op0=ALU.max, op1=ALU.min,
                                        accum_out=minsq[b][:, cj:cj + 1])

        def sqrt_(b, cj):
            if added_in_psum(b, cj):
                nc.scalar.activation(out=F[b][:, cj, :], in_=F[b][:, cj, :], func=ACT.Sqrt,
                                     bias=k2[b][:, cj:cj + 1])
            else:
                nc.scalar.activation(out=F[b][:, cj, :], in_=F[b][:, cj, :], func=ACT.Sqrt)

        def min_sqrt(b):
            n = 8 - QA[b]
            nc.vector.tensor_reduce(out=minsq[b][:, n:8], in_=minh[b][:, n:8, :], axis=AX.X, op=ALU.min)
            nc.scalar.activation(out=mn[b][:, 0:n], in_=minsq[b][:, 0:n], func=ACT.Sqrt)
            for cj in range(n, 8):
                nc.scalar.activation(out=mn[b][:, cj:cj + 1], in_=minsq[b][:, cj:cj + 1], func=ACT.Sqrt,
                                     bias=k2[b][:, cj:cj + 1])

        def expo(b, cj):
            nc.scalar.activation(out=F[b][:, cj, :], in_=F[b][:, cj, :], func=ACT.Exp,
                                 bias=mn[b][:, cj:cj + 1], scale=-1.0,
                                 accum_out=first[b][:, cj:cj + 1])

        def hi(b, cj):
            nc.vector.tensor_copy(out=TH[b][:, cj, :], in_=F[b][:, cj, :])

        def lo(b, cj):
            nc.vector.tensor_tensor(out=TL[b][:, cj, :], in0=F[b][:, cj, :], in1=TH[b][:, cj, :],
                                    op=ALU.subtract)

        def hilo_gpsimd(b, cj):
            nc.gpsimd.tensor_scalar(out=TH[b][:, cj, :], in0=F[b][:, cj, :], scalar1=1.0,
                                    scalar2=0.0, op0=ALU.mult, op1=ALU.add)
            nc.gpsimd.tensor_tensor(out=TL[b][:, cj, :], in0=F[b][:, cj, :], in1=TH[b][:, cj, :],
                                    op=ALU.subtract)

        def v_first(b):
            v_new(b)
            v_rec(b, first[b], 0, 8)
            v_lo(b, 0, 8)

        def v_rec(b, src, j0, j1):
            nc.vector.reciprocal(out=vcur[b][:, j0:j1], in_=src[:, j0:j1])
            with nc.allow_low_precision(reason="the bf16 head of v; its tail goes into the second column"):
                nc.vector.reciprocal(out=vsp[b][:, j0:j1, 0], in_=src[:, j0:j1])

        def v_lo(b, j0, j1):
            nc.vector.tensor_tensor(out=vsp[b][:, j0:j1, 1], in0=vcur[b][:, j0:j1], in1=vsp[b][:, j0:j1, 0],
                                    op=ALU.subtract)

        def v_new(b):
            vcur[b] = small.tile([P, 8], F32, name="v%d" % b, tag="v%d" % b)
            vsp[b] = small.tile([P, 8, 2], BF16, name="vsp%d" % b, tag="vsp%d" % b)

        def v_red(b, j0, j1):
            nc.vector.tensor_reduce(out=sums[b][:, j0:j1], in_=halves[b][:, j0:j1, :], axis=AX.X, op=ALU.add)

        def g_open(b):
            bank[b] = psum.tile([P, 512], F32, name="R", tag="mv%d" % b, bufs=1)
            nc.tensor.matmul(out=bank[b][:, 0:16], lhsT=ident_bf[:], rhs=zeros[:], start=True, stop=False)

        def keep_clock(b, passes):
            for n in range(passes):
                nc.tensor.matmul_mx(out=bank[b][:], lhsT=vc[0][:, 0:P].bitcast(FP8X4), lhsT_scale=vs_[0][:, 0:P],
                                    rhs=wc[:].bitcast(FP8X4), rhs_scale=ws[:], start=True, stop=True)

        def g_tiles(b, j0, j1):
            for cj in range(j0, j1):
                for s, piece in enumerate((TH[b], TL[b])):
                    for i in range(8):
                        nc.tensor.matmul(out=bank[b][:, 2 * i:2 * i + 2], lhsT=piece[:, cj, P * i:P * i + P],
                                         rhs=vsp[b][:, cj, :],
                                         start=False, stop=(cj == 7 and s == 1 and i == 7))

        def u_red(b):
            rcur[b] = small.tile([P, 8], F32, name="r%d" % b, tag="r%d" % b)
            nc.vector.tensor_reduce(out=rcur[b][:], in_=bank[b][:, 0:16].rearrange("p (i k) -> p i k", k=2), axis=AX.X,
                                    op=ALU.add)

        def u_rec(b):
            ucur[b] = small.tile([P, 8], F32, name="u%d" % b, tag="u%d" % b)
            nc.vector.reciprocal(out=ucur[b][:], in_=rcur[b][:])
            for hh in range(2):
                ub[b][hh] = spread_half(ucur[b], hh, "qk", 4)

        def u_copy(b, hh):
            if ubs[0] is None:
                ubs[0] = big.tile([P, B, T], F32, name="ubs", tag="sY", align_bytes=64)
            if True:
                nc.scalar.copy(out=ubs[0][:, b, 512 * hh:512 * hh + 512], in_=ub[b][hh][:])

        def f_side(b):
            for cj in range(NV, 8):
                prod = scr.tile([P, T], F32, name="prod", tag="prod", bufs=2)
                nc.gpsimd.tensor_tensor(out=prod[:], in0=F[b][:, cj, :], in1=ubs[0][:, b, :], op=ALU.mult)
                nc.scalar.activation(out=prod[:], in_=prod[:], func=ACT.Copy,
                                     accum_out=sums[b][:, cj:cj + 1])

        def f_vec(b, k):
            cj, hh = k // 2, k % 2
            if k == 0:
                halves[b] = small.tile([P, NV, 2], F32, name="halves%d" % b, tag="halves%d" % b)
            junk = scr.tile([P, 512], F32, name="junk", tag="junk", bufs=3)
            nc.vector.scalar_tensor_tensor(
                out=junk[:], in0=F[b][:, cj, 512 * hh:512 * hh + 512], scalar=1.0,
                in1=ub[b][hh][:], op0=ALU.mult, op1=ALU.mult,
                accum_out=halves[b][:, cj, hh:hh + 1])

        wc = const.tile([P, D], U32, name="wc", align_bytes=64)
        ws = const.tile([P, D], U8, name="ws", align_bytes=64)
        vpc = [const.tile([P, 2, D], U32, name="vpc%d" % b, align_bytes=64) for b in range(B)]
        vps = [const.tile([P, 2, D], U8, name="vps%d" % b, align_bytes=64) for b in range(B)]
        vg = [None, None]
        vc = [None, None]
        vs_ = [None, None]
        vpg = [None, None]

        def v_load(b):
            v_raw[b] = big.tile([P, 8, D], BF16, name="v_raw%d" % b, tag=("sA", "sE")[b], align_bytes=64)
            nc.sync.dma_start(out=v_raw[b][:].rearrange("p (c j) d -> p c j d", c=2),
                              in_=v[b].rearrange("(c p j) d -> p c j d", c=2, j=4))

        def v_tr(b, g):
            vw = v_raw[b][:].bitcast(F32)
            if g == 0:
                vg[b] = big.tile([P, N, 4], BF16, name="vg", tag=("sY", "sC")[b], align_bytes=64)
            vgw = vg[b][:].bitcast(F32)
            pv = psum.tile([P, 2, 2, P], F32, name="pv", tag="tr", bufs=2)
            for a in range(2):
                for u in range(2):
                    nc.tensor.transpose(out=pv[:, a, u, :],
                                        in_=vw[:, 2 * g + a, P * u:P * u + P],
                                        identity=ident_f[:])
            nc.scalar.copy(
                out=vgw[:, 256 * g:256 * g + 256, :].rearrange("p (a n) u -> p a n u", a=2),
                in_=pv[:].rearrange("p a u n -> p a n u"))

        def v_quant(b):
            vc[b] = big.tile([P, N], U32, name="vc", tag="vc%d" % b, align_bytes=64)
            vs_[b] = big.tile([P, N], U8, name="vs_", tag="vs_%d" % b, align_bytes=64)
            nc.vector.quantize_mx(out=vc[b][:].bitcast(FP8X4), scales=vs_[b][:],
                                  in_=vg[b][:].rearrange("p n t -> p (n t)"))

        def vp_piece(b, k):
            c, eq = k // 4, k % 4
            if k == 0:
                vpg[b] = big.tile([P, 2, D, 4], BF16, name="vpg", tag=("sD", "sF")[b], align_bytes=64)
            pvp = psum.tile([P, 4, P], F32, name="pvp", tag="tr", bufs=2)
            for j in range(4):
                cj = 4 * c + j
                nc.tensor.matmul_mx(
                    out=pvp[:, j, :],
                    lhsT=vc[b][:, P * cj:P * cj + P].bitcast(FP8X4),
                    lhsT_scale=vs_[b][:, P * cj:P * cj + P],
                    rhs=wc[:, P * eq:P * eq + P].bitcast(FP8X4),
                    rhs_scale=ws[:, P * eq:P * eq + P],
                    start=True, stop=True)
            nc.scalar.copy(out=vpg[b][:, c, P * eq:P * eq + P, :],
                           in_=pvp[:].rearrange("p j e -> p e j"))

        def vp_quant(b):
            nc.vector.quantize_mx(out=vpc[b][:].rearrange("p c e -> p (c e)").bitcast(FP8X4),
                                  scales=vps[b][:].rearrange("p c e -> p (c e)"),
                                  in_=vpg[b][:].rearrange("p c e j -> p (c e j)"))

        for i in range(4):
            q_norm(i)
            q_tr(i)
        for cj in range(4):
            k_tr(0, cj)
            k_norm(0, cj)
        q2_spread(0)
        for i in range(4, 8):
            q_norm(i)
        mm(0, 0, 0)
        mm(0, 1, 0)
        for i in range(4, 8):
            q_tr(i)
        v_load(0)
        mm(0, 2, 0)
        mm(0, 3, 0)
        q2_spread(1)
        for cj in range(4, 8):
            k_norm(0, cj)
        for cj in range(8):
            k_norm(1, cj)
        for cj in range(4):
            mm(0, cj, 1)
            k_tr(0, 4 + cj)
            if cj > 0:
                clamp(0, cj - 1)
                sqrt_(0, cj - 1)
        w_raw = big.tile([P, 4, D], BF16, name="w_raw", tag="sB", align_bytes=64)
        nc.sync.dma_start(out=w_raw[:].rearrange("p (u e) c -> p u e c", u=2),
                          in_=w_v.rearrange("(u q e) c -> q u e c", u=2, e=2))
        wg = big.tile([P, D, 4], BF16, name="wg", tag="sX", align_bytes=64)
        nc.gpsimd.tensor_scalar(out=wg[:], in0=w_raw[:].rearrange("p t c -> p c t"), scalar1=1.0,
                                scalar2=0.0, op0=ALU.mult, op1=ALU.add)
        floors(0)
        for cj in range(4, 8):
            mm(0, cj, 0)
            clamp(0, cj - 1)
            sqrt_(0, cj - 1)
            mm(0, cj, 1)
            if cj >= 6:
                k_tr(1, 2 * (cj - 6))
                k_tr(1, 2 * (cj - 6) + 1)
            v_tr(0, cj - 4)
        clamp(0, 7)
        sqrt_(0, 7)
        min_sqrt(0)
        v_load(1)

        for cj in range(8):
            expo(0, cj)
        floors(1)
        v_quant(0)
        nc.vector.quantize_mx(out=wc[:].bitcast(FP8X4), scales=ws[:],
                              in_=wg[:].rearrange("p c t -> p (c t)"))
        for cj in range(8):
            mm(1, cj, 0)
            if cj > 0:
                clamp(1, cj - 1)
                sqrt_(1, cj - 1)
            if cj < 4:
                k_tr(1, 4 + cj)
            mm(1, cj, 1)
            if cj < SPLIT_GPSIMD:
                hilo_gpsimd(0, cj)
        clamp(1, 7)
        sqrt_(1, 7)
        min_sqrt(1)
        for cj in range(SPLIT_GPSIMD, 8):
            hi(0, cj)
            if cj > SPLIT_GPSIMD:
                lo(0, cj - 1)
        lo(0, 7)
        v_first(0)
        for cj in range(8):
            expo(1, cj)
        g_open(0)
        g_tiles(0, 0, 8)
        for cj in GHL1:
            hilo_gpsimd(1, cj)
        for cj in SHI1:
            nc.scalar.copy(out=TH[1][:, cj, :], in_=F[1][:, cj, :])
        for k in range(4):
            vp_piece(0, k)
        ops = []
        wait = []
        for cj in range(8):
            if cj not in GHL1:
                if cj not in SHI1:
                    ops.append(lambda cj=cj: hi(1, cj))
                if wait:
                    ops.append(wait.pop(0))
                wait.append(lambda cj=cj: lo(1, cj))
        ops.extend(wait)
        for n, op in enumerate(ops):
            if n == len(ops) - 3:
                u_red(0)
            if n == len(ops) - 2:
                u_rec(0)
            op()
        v_first(1)
        keep_clock(0, K0)
        g_open(1)
        for cj in range(8):
            g_tiles(1, cj, cj + 1)
            if cj in PG1:
                keep_clock(0, 1)

        def w_scalar(b, tiles):
            for cj in tiles:
                nc.scalar.activation(out=F[b][:, cj, :], in_=F[b][:, cj, :], func=ACT.Copy,
                                     scale=vcur[b][:, cj:cj + 1])

        def w_gpsimd(b, tiles):
            for cj in tiles:
                nc.gpsimd.tensor_scalar(out=F[b][:, cj, :], in0=F[b][:, cj, :],
                                        scalar1=vcur[b][:, cj:cj + 1], scalar2=0.0,
                                        op0=ALU.mult, op1=ALU.add)

        vp_todo = list(range(4, 16))

        def late(b):
            for cj in range(EARLY, 8):
                g_tiles(b, cj, cj + 1)
                if cj in PGA:
                    keep_clock(1 - b, 1)

        def slot(x, y, step):
            last = step == STEPS - 1
            for k in range(2 * NV):
                f_vec(x, k)
                if k < 2:
                    u_copy(x, k)
                if k == 1 and step > 0:
                    v_rec(y, sums[y], EARLY, 8)
                if k == 1:
                    if last:
                        w_scalar(y, (0, 1, 2))
                    if step < 2:
                        v_tr(1, 2 * step)
                        v_tr(1, 2 * step + 1)
                    if not last:
                        e = vp_todo.pop(0)
                        vp_piece(e // 8, e % 8)
                    f_side(x)
                if step > 0:
                    if k == 0:
                        v_red(y, EARLY, NV)
                    if k == 2:
                        v_lo(y, EARLY, 8)
                        late(y)
                        keep_clock(x, D2)
                if k == KQ and step == 3:
                    v_quant(1)
                if k == KU:
                    u_red(y)
                if k == KU + 1:
                    u_rec(y)
                if k == KV:
                    v_new(x)
                    v_red(x, 0, EARLY)
                if k == KV + 1:
                    v_rec(x, sums[x], 0, EARLY)
                if k == KV + 2:
                    v_lo(x, 0, EARLY)
                    keep_clock(y, D0)
                    g_open(x)
                    for cj in range(EARLY):
                        g_tiles(x, cj, cj + 1)
                        if cj in PGA:
                            keep_clock(y, 1)
                    keep_clock(y, D1)

        for step in range(STEPS):
            slot(step % 2, 1 - step % 2, step)

        pis = big.tile([P, B, 2, T], U8, name="pis", tag="sG", align_bytes=64)
        pig = [None, None]
        pic = [None, None]

        def pi_tiles(b):
            pig[b] = big.tile([P, 2, T, 4], BF16, name="pig", tag="th%d" % b, align_bytes=64)
            pic[b] = big.tile([P, 2, T], U32, name="pic", tag="tl%d" % b, align_bytes=64)

        def pi_mul(b, h, c):
            sl = slice(512 * h, 512 * h + 512)
            nc.vector.tensor_tensor(
                out=pig[b][:, c, sl, :].rearrange("p (g i) j -> p g j i", i=4),
                in0=F[b][:, 4 * c:4 * c + 4, sl].rearrange("p j (g i) -> p g j i", i=4),
                in1=ub[b][h][:].rearrange("p (g i) -> p g i", i=4).unsqueeze(2).to_broadcast([P, 128, 4, 4]),
                op=ALU.mult)

        def pi_mul_gpsimd(b, c, parts):
            w = 512 // parts
            for p in range(parts):
                sl = slice(512 + w * p, 512 + w * p + w)
                nc.gpsimd.tensor_tensor(
                    out=pig[b][:, c, sl, :].rearrange("p (g i) j -> p g j i", i=4),
                    in0=F[b][:, 4 * c:4 * c + 4, sl].rearrange("p j (g i) -> p g j i", i=4),
                    in1=ubs[0][:, b, sl].rearrange("p (g i) -> p g i", i=4).unsqueeze(2).to_broadcast([P, w // 4, 4, 4]),
                    op=ALU.mult)

        def pi_quant(b, h, cs=(0, 1)):
            sl = slice(512 * h, 512 * h + 512)
            for c in cs:
                nc.vector.quantize_mx(out=pic[b][:, c, sl].bitcast(FP8X4), scales=pis[:, b, c, sl],
                                      in_=pig[b][:, c, sl, :].rearrange("p t j -> p (t j)"))

        def out_half(b, h):
            ov = out[b].rearrange("(p i) d -> p i d", i=8)
            last = b == 1 and h == 1
            for a2 in range(2):
                ost = big.tile([P, 2, D], F32, name="ost", tag=("sA", "sE", "sB", "sC")[2 * h + a2],
                               align_bytes=64)
                for a in range(2):
                    i = 4 * h + 2 * a2 + a
                    po = psum.tile([P, D], F32, name="po", tag="tr", bufs=2)
                    for c in range(2):
                        nc.tensor.matmul_mx(
                            out=po[:],
                            lhsT=pic[b][:, c, P * i:P * i + P].bitcast(FP8X4),
                            lhsT_scale=pis[:, b, c, P * i:P * i + P],
                            rhs=vpc[b][:, c, :].bitcast(FP8X4),
                            rhs_scale=vps[b][:, c, :],
                            start=(c == 0), stop=(c == 1))
                    if last and a == 1:
                        nc.vector.tensor_copy(out=ost[:, a, :], in_=po[:])
                    else:
                        nc.scalar.copy(out=ost[:, a, :], in_=po[:])
                    if last:
                        nc.sync.dma_start(out=ov[:, i, :], in_=ost[:, a, :])
                i0 = 4 * h + 2 * a2
                if not last:
                    nc.sync.dma_start(out=ov[:, i0:i0 + 2, :], in_=ost[:])

        pi_tiles(0)
        w_gpsimd(0, (3, 5, 7))
        nc.scalar.copy(out=ubs[0][:, 0, 512:1024], in_=ub[0][1][:])
        w_scalar(0, (4, 6))
        v_red(1, EARLY, NV)
        pi_mul(0, 0, 0)
        v_rec(1, sums[1], EARLY, 8)
        v_lo(1, EARLY, 8)
        late(1)
        w_scalar(1, WS1)
        w_gpsimd(1, WG1)
        while vp_todo:
            e = vp_todo.pop(0)
            vp_piece(e // 8, e % 8)
        pi_tiles(1)
        pi_mul_gpsimd(0, 1, 2)
        pi_mul(0, 0, 1)
        u_red(1)
        vp_quant(0)
        u_rec(1)
        nc.scalar.copy(out=ubs[0][:, 1, 512:1024], in_=ub[1][1][:])
        pi_mul_gpsimd(1, 1, 2)
        pi_quant(0, 0)
        out_half(0, 0)
        pi_mul(0, 1, 0)
        pi_quant(0, 1, (0,))
        pi_mul(1, 0, 0)
        pi_quant(0, 1, (1,))
        out_half(0, 1)
        pi_mul(1, 0, 1)
        vp_quant(1)
        pi_quant(1, 0)
        out_half(1, 0)
        pi_mul(1, 1, 0)
        pi_quant(1, 1)
        out_half(1, 1)
